import numpy as np
import ml_dtypes


def mxq(x, axis, fmt="e4m3"):
    dtype, down = {"e4m3": (ml_dtypes.float8_e4m3fn, 7), "e5m2": (ml_dtypes.float8_e5m2, 14)}[fmt]
    v = np.moveaxis(np.asarray(x, np.float32).astype(ml_dtypes.bfloat16).astype(np.float64), axis, -1)
    blocks = v.reshape(v.shape[:-1] + (-1, 32))
    amax = np.abs(blocks).max(-1, keepdims=True)
    byte = np.maximum(np.where(amax > 0, np.frexp(amax)[1] - 1 + 127, 0) - down, 1)
    scale = np.exp2(byte - 127.0)
    codes = (blocks / scale).astype(np.float32).astype(dtype).astype(np.float64)
    return np.moveaxis((codes * scale).reshape(v.shape), -1, axis)


WIDE = False


def mx_kscale(k):
    if not WIDE:
        return np.ones(k)
    levels = np.array([10, -10, 5, -5, 0])
    a = np.random.permutation(np.resize(levels, k // 512 * 4)).reshape(k // 512, 4)
    idx = np.arange(k)
    return np.exp2(a[idx // 512, idx % 128 // 32])


BF16 = ml_dtypes.bfloat16


def bf(x):
    return np.asarray(x, np.float32).astype(BF16)


def f64(x):
    return np.asarray(x).astype(np.float64)


B, CIN, H, W, CR, COUT, SP, K = 4, 2048, 8, 8, 512, 2048, 8, 7
PAD = K // 2
KK = K * K
HN = COUT // SP
HW = H * W
OFFS = [(dy, dx) for dy in range(K) for dx in range(K)]


def setup_inputs():
    s = mx_kscale(CIN)
    return {
        "logits": bf(np.random.standard_normal((B, HN, KK, HW)) * 1.5),
        "x": bf(np.random.standard_normal((B, CIN, H, W)) * s[None, :, None, None]),
        "w3c": bf(np.random.standard_normal((COUT, CIN)) * 2.0 / np.sqrt(CIN) / s[None, :]),
        "b3c": bf(np.random.standard_normal(COUT) * 0.5),
    }


def reference(logits, x, w3c, b3c):
    x3 = (mxq(f64(w3c), 1, "e4m3") @ mxq(f64(x).reshape(B, CIN, HW), 1, "e4m3")) + f64(b3c)[None, :, None]
    x3 = x3.reshape(B, COUT, H, W)
    lg = f64(logits)
    e = np.exp(lg - lg.max(axis=2, keepdims=True))
    wgt = (e / e.sum(axis=2, keepdims=True)).reshape(B, HN, KK, H, W)
    x3p = np.pad(x3, ((0, 0), (0, 0), (PAD, PAD), (PAD, PAD)), mode="reflect")
    acc = np.zeros((B, HN, SP, H, W))
    for k, (dy, dx) in enumerate(OFFS):
        patch = x3p[:, :, dy:dy + H, dx:dx + W].reshape(B, HN, SP, H, W)
        acc = acc + patch * wgt[:, :, k][:, :, None]
    return acc.reshape(B, COUT, H, W)

@@ -1,0 +1,239 @@
+from contextlib import ExitStack
+
+import concourse.mybir as mybir
+from concourse.masks import make_identity
+
+F32 = mybir.dt.float32
+BF16 = mybir.dt.bfloat16
+U32 = mybir.dt.uint32
+U8 = mybir.dt.uint8
+FP8X4 = mybir.dt.float8_e4m3fn_x4
+ALU = mybir.AluOpType
+ACT = mybir.ActivationFunctionType
+
+P = 128
+SIDE = 8
+TAPS = 7
+REACH = TAPS // 2
+PITCH = TAPS + REACH + 1
+FLOPS = 2 * 2048 * 2048 * 256 + 2 * 4 * 2048 * 64 * 49
+
+
+def mirrored(u):
+    if u < 0:
+        return -u
+    if u > SIDE - 1:
+        return 2 * (SIDE - 1) - u
+    return u
+
+
+def tile_sam_pb_kernel(tc, logits, x, w3c, b3c, out):
+    nc = tc.nc
+    with ExitStack() as stack:
+        keep = stack.enter_context(tc.tile_pool(name="keep", bufs=1))
+        loads = stack.enter_context(tc.tile_pool(name="loads", bufs=2))
+        ends = stack.enter_context(tc.tile_pool(name="ends", bufs=2))
+        psum = stack.enter_context(tc.psum_pool(name="psum", bufs=2))
+
+        ident = keep.tile([P, P], F32)
+        make_identity(nc, ident[:])
+
+        padded = keep.tile([P, 2, TAPS, SIDE * PITCH, SIDE], F32)
+        nc.vector.memset(padded[:], 0.0)
+        shifted = [keep.tile([P, SIDE, 2, SIDE, SIDE], F32, name="shifted%d" % i) for i in range(SIDE)]
+        for i in range(SIDE):
+            nc.vector.memset(shifted[i][:], 0.0)
+
+        def build_weights(hh, t):
+            lt = loads.tile([P, 2, TAPS * TAPS, SIDE * SIDE], BF16)
+            for gl in range(2):
+                nc.sync.dma_start(out=lt[:, gl], in_=logits[2 * t + gl, hh * P : (hh + 1) * P])
+            top = keep.tile([P, 2, 24, SIDE * SIDE], BF16)
+            nc.vector.tensor_tensor(out=top[:], in0=lt[:, :, 0:24, :], in1=lt[:, :, 24:48, :], op=ALU.max)
+            width = 24
+            while width > 1:
+                half = width // 2
+                nc.vector.tensor_tensor(
+                    out=top[:, :, 0:half, :],
+                    in0=top[:, :, 0:half, :],
+                    in1=top[:, :, width - half : width, :],
+                    op=ALU.max,
+                )
+                width -= half
+            nc.vector.tensor_tensor(out=top[:, :, 0, :], in0=top[:, :, 0, :], in1=lt[:, :, 48, :], op=ALU.max)
+
+            taps = lt[:].rearrange("p gl (dy dx) (i j) -> p gl dy dx i j", dx=TAPS, j=SIDE)
+            tops = top[:, :, 0, :].rearrange("p gl (i j) -> p gl i j", j=SIDE)
+            for gl in range(2):
+                for j in range(SIDE):
+                    nc.gpsimd.tensor_tensor(
+                        out=padded[:, gl, :, PITCH * j : PITCH * j + TAPS, :],
+                        in0=taps[:, gl, :, :, :, j],
+                        in1=tops[:, gl, :, j].unsqueeze(1).unsqueeze(1).to_broadcast([P, TAPS, TAPS, SIDE]),
+                        op=ALU.subtract,
+                    )
+                live = padded[:, gl].rearrange("p dy (j s) i -> p dy j (s i)", s=PITCH)[:, :, :, 0 : TAPS * SIDE]
+                nc.scalar.activation(out=live, in_=live, func=ACT.Exp)
+
+            for j in range(SIDE):
+                for dx in range(TAPS):
+                    u = j + dx - REACH
+                    if mirrored(u) != u:
+                        target = padded[:, :, :, PITCH * j + mirrored(u) - j + REACH, :]
+                        nc.vector.tensor_tensor(
+                            out=target, in0=target, in1=padded[:, :, :, PITCH * j + dx, :], op=ALU.add
+                        )
+
+            for i in range(SIDE):
+                skew = padded[:, :, :, REACH : REACH + SIDE * (PITCH - 1), i].rearrange(
+                    "p gl dy (j s) -> p j gl dy s", s=PITCH - 1
+                )[:, :, :, :, 0:SIDE]
+                first = max(0, REACH - i)
+                last = min(TAPS - 1, SIDE - 1 + REACH - i)
+                nc.vector.tensor_copy(
+                    out=shifted[i][:, :, :, first + i - REACH : last + i - REACH + 1, :],
+                    in_=skew[:, :, :, first : last + 1, :],
+                )
+                for dy in range(TAPS):
+                    u = i + dy - REACH
+                    if mirrored(u) != u:
+                        row = shifted[i][:, :, :, mirrored(u), :]
+                        nc.vector.tensor_tensor(out=row, in0=row, in1=skew[:, :, :, dy, :], op=ALU.add)
+
+        build_weights(0, 0)
+
+        bias_bf = keep.tile([P, 2, 8], BF16)
+        nc.sync.dma_start(out=bias_bf[:], in_=b3c.rearrange("(hh k c) -> k hh c", hh=2, k=P, c=8))
+        bias = keep.tile([P, 2, 8], F32)
+        nc.vector.tensor_copy(out=bias[:], in_=bias_bf[:])
+
+        codes_x = keep.tile([P, 1024], U32, align_bytes=64)
+        scales_x = keep.tile([P, 1024], U8, align_bytes=64)
+        x3 = keep.tile([P, 2, 256, 9], F32)
+        nc.vector.memset(x3[:, :, :, 8:9], 1.0)
+
+        with tc.tile_pool(name="once", bufs=1) as once, tc.tile_pool(name="stream", bufs=2) as stream:
+            raw_x = once.tile([P, 32, 128], BF16)
+            nc.sync.dma_start(
+                out=raw_x[:],
+                in_=x.rearrange("b (g u p e) i j -> p (b g u) (e i j)", g=4, u=2, p=P, e=2),
+            )
+            grouped_x = once.tile([P, 2, 4, 2, 64, 4], BF16, align_bytes=64)
+            raw_view = raw_x[:].rearrange(
+                "p (t gl g u) (e n) -> p t g gl n (u e)", t=2, gl=2, g=4, u=2, e=2
+            )
+            for t in range(2):
+                nc.vector.tensor_copy(out=grouped_x[:, t], in_=raw_view[:, t])
+            nc.vector.quantize_mx(
+                out=codes_x[:].bitcast(FP8X4),
+                scales=scales_x[:],
+                in_=grouped_x[:].rearrange("p t g gl n f -> p (t g gl n f)"),
+            )
+
+            for ot in range(8):
+                w_sb = stream.tile([P, 2, 2048], BF16)
+                nc.sync.dma_start(
+                    out=w_sb[:],
+                    in_=w3c[ot * 256 : (ot + 1) * 256, :].rearrange("(ob p) k -> p ob k", p=P),
+                )
+                grouped_w = stream.tile([P, 4, 256, 4], BF16, align_bytes=64)
+                for g in range(4):
+                    wt = psum.tile([P, 2, 256], F32, tag="turned", bufs=4)
+                    for u in range(2):
+                        for ob in range(2):
+                            words = w_sb[:, ob, :].bitcast(F32)
+                            nc.tensor.transpose(
+                                wt[:, u, ob * P : (ob + 1) * P],
+                                words[:, (2 * g + u) * P : (2 * g + u + 1) * P],
+                                ident[:],
+                            )
+                    nc.scalar.copy(out=grouped_w[:, g].bitcast(F32), in_=wt[:].rearrange("p u o -> p o u"))
+                codes_w = stream.tile([P, 4, 256], U32, align_bytes=64)
+                scales_w = stream.tile([P, 4, 256], U8, align_bytes=64)
+                nc.vector.quantize_mx(
+                    out=codes_w[:].rearrange("p g o -> p (g o)").bitcast(FP8X4),
+                    scales=scales_w[:].rearrange("p g o -> p (g o)"),
+                    in_=grouped_w[:].rearrange("p g o f -> p (g o f)"),
+                )
+                acc = psum.tile([P, 2, 256], F32, tag="sums")
+                for t in range(2):
+                    for g in range(4):
+                        cols = slice((t * 4 + g) * P, (t * 4 + g + 1) * P)
+                        nc.tensor.matmul_mx(
+                            out=acc[:, t, :],
+                            lhsT=codes_x[:, cols].bitcast(FP8X4),
+                            lhsT_scale=scales_x[:, cols],
+                            rhs=codes_w[:, g, :].bitcast(FP8X4),
+                            rhs_scale=scales_w[:, g, :],
+                            start=(g == 0),
+                            stop=(g == 3),
+                        )
+                nc.scalar.copy(
+                    out=x3[:, :, ot * 32 : (ot + 1) * 32, 0:8],
+                    in_=acc[:].rearrange("p t (h c) -> p t h c", c=8),
+                )
+
+        wide = stack.enter_context(tc.tile_pool(name="wide", bufs=1))
+        window = wide.tile([P, P, P], F32)
+        nc.vector.memset(window[0:64, :, 64:128], 0.0)
+        nc.gpsimd.memset(window[64:128, :, 0:64], 0.0)
+
+        out_view = out.rearrange("b (hh k c) i j -> b hh k (c i j)", hh=2, k=P, c=8)
+        chunks = [(hh, t) for hh in range(2) for t in range(2)]
+        for index, (hh, t) in enumerate(chunks):
+            for i in range(SIDE):
+                for jh in range(2):
+                    turned = psum.tile([P, 4, P], F32, tag="turned", bufs=4)
+                    for s in range(4):
+                        nc.tensor.transpose(
+                            turned[:, s, :],
+                            shifted[i][:, 4 * jh + s].rearrange("p gl mi mj -> p (gl mi mj)"),
+                            ident[:],
+                        )
+                    n0 = SIDE * i + 4 * jh
+                    nc.vector.tensor_copy(
+                        out=window[0:64, :, n0 : n0 + 4], in_=turned[0:64].rearrange("p s k -> p k s")
+                    )
+                    nc.scalar.copy(
+                        out=window[64:128, :, 64 + n0 : 64 + n0 + 4],
+                        in_=turned[64:128].rearrange("p s k -> p k s"),
+                    )
+            if index + 1 < len(chunks):
+                build_weights(*chunks[index + 1])
+
+            normed = ends.tile([P, 8, P], F32)
+            for kb in range(4):
+                sums = psum.tile([P, 32, 9], F32, tag="sums")
+                for kk in range(32):
+                    k = kb * 32 + kk
+                    nc.tensor.matmul(
+                        out=sums[:, kk, :],
+                        lhsT=window[:, k, :],
+                        rhs=x3[:, t, hh * P + k, :],
+                        start=True,
+                        stop=True,
+                    )
+                rec = ends.tile([P, 32, 1], F32)
+                nc.vector.reciprocal(out=rec[:], in_=sums[:, :, 8:9])
+                nc.vector.tensor_tensor(
+                    out=normed[:, :, kb * 32 : (kb + 1) * 32],
+                    in0=sums[:, :, 0:8].rearrange("p k c -> p c k"),
+                    in1=rec[:].rearrange("p k o -> p o k").to_broadcast([P, 8, 32]),
+                    op=ALU.mult,
+                )
+            result = ends.tile([P, 2, 8, 64], F32)
+            for half in range(2):
+                flipped = psum.tile([P, 4, P], F32, tag="flipped")
+                for cc in range(4):
+                    nc.tensor.transpose(flipped[:, cc, :], normed[:, half * 4 + cc, :], ident[:])
+                nc.vector.tensor_tensor(
+                    out=result[:, :, half * 4 : (half + 1) * 4, :].rearrange("p gl c n -> p c gl n"),
+                    in0=flipped[:].rearrange("p c (gl n) -> p c gl n", gl=2),
+                    in1=bias[:, hh, half * 4 : (half + 1) * 4]
+                    .unsqueeze(2)
+                    .unsqueeze(3)
+                    .to_broadcast([P, 4, 2, 64]),
+                    op=ALU.add,
+                )
+            for gl in range(2):
+                nc.sync.dma_start(out=out_view[2 * t + gl, hh], in_=result[:, gl].rearrange("p c n -> p (c n)"))

@@ -13,9 +13,11 @@ ACT = mybir.ActivationFunctionType
 
 P = 128
 SIDE = 8
+SPOTS = SIDE * SIDE
 TAPS = 7
 REACH = TAPS // 2
-PITCH = TAPS + REACH + 1
+WIDE = SIDE + 2 * REACH
+SHARE = 8
 FLOPS = 2 * 2048 * 2048 * 256 + 2 * 4 * 2048 * 64 * 49
 
 
@@ -32,23 +34,32 @@ def tile_sam_pb_kernel(tc, logits, x, w3c, b3c, out):
     with ExitStack() as stack:
         keep = stack.enter_context(tc.tile_pool(name="keep", bufs=1))
         loads = stack.enter_context(tc.tile_pool(name="loads", bufs=2))
+        stream = stack.enter_context(tc.tile_pool(name="stream", bufs=2))
         ends = stack.enter_context(tc.tile_pool(name="ends", bufs=2))
         psum = stack.enter_context(tc.psum_pool(name="psum", bufs=2))
 
         ident = keep.tile([P, P], F32)
         make_identity(nc, ident[:])
+        exchange = keep.tile([P, P], F32)
+        nc.vector.tensor_copy(out=exchange[:, 0:SPOTS], in_=ident[:, SPOTS:P])
+        nc.vector.tensor_copy(out=exchange[:, SPOTS:P], in_=ident[:, 0:SPOTS])
 
-        padded = keep.tile([P, 2, TAPS, SIDE * PITCH, SIDE], F32)
-        nc.vector.memset(padded[:], 0.0)
-        shifted = [keep.tile([P, SIDE, 2, SIDE, SIDE], F32, name="shifted%d" % i) for i in range(SIDE)]
-        for i in range(SIDE):
-            nc.vector.memset(shifted[i][:], 0.0)
+        weights = [keep.tile([P, 2, TAPS * TAPS + 1, SPOTS], F32, name="weights%d" % r) for r in range(2)]
+        for r in range(2):
+            nc.vector.memset(weights[r][:, :, TAPS * TAPS :, :], 0.0)
+        products = [
+            [keep.tile([P, SHARE, SIDE, SIDE], F32, name="products%d_%d" % (dy, r)) for r in range(2)]
+            for dy in range(TAPS)
+        ]
+        for dy in range(TAPS):
+            for r in range(2):
+                nc.vector.memset(products[dy][r][:], 0.0)
 
-        def build_weights(hh, t):
-            lt = loads.tile([P, 2, TAPS * TAPS, SIDE * SIDE], BF16)
+        def softmax_numerators(hh, t, e):
+            lt = loads.tile([P, 2, TAPS * TAPS, SPOTS], BF16)
             for gl in range(2):
                 nc.sync.dma_start(out=lt[:, gl], in_=logits[2 * t + gl, hh * P : (hh + 1) * P])
-            top = keep.tile([P, 2, 24, SIDE * SIDE], BF16)
+            top = keep.tile([P, 2, 24, SPOTS], BF16)
             nc.vector.tensor_tensor(out=top[:], in0=lt[:, :, 0:24, :], in1=lt[:, :, 24:48, :], op=ALU.max)
             width = 24
             while width > 1:
@@ -60,90 +71,64 @@ def tile_sam_pb_kernel(tc, logits, x, w3c, b3c, out):
                     op=ALU.max,
                 )
                 width -= half
-            nc.vector.tensor_tensor(out=top[:, :, 0, :], in0=top[:, :, 0, :], in1=lt[:, :, 48, :], op=ALU.max)
-
-            taps = lt[:].rearrange("p gl (dy dx) (i j) -> p gl dy dx i j", dx=TAPS, j=SIDE)
-            tops = top[:, :, 0, :].rearrange("p gl (i j) -> p gl i j", j=SIDE)
+            nc.vector.tensor_tensor(
+                out=top[:, :, 0:1, :], in0=top[:, :, 0:1, :], in1=lt[:, :, 48:49, :], op=ALU.max
+            )
             for gl in range(2):
-                for j in range(SIDE):
-                    nc.gpsimd.tensor_tensor(
-                        out=padded[:, gl, :, PITCH * j : PITCH * j + TAPS, :],
-                        in0=taps[:, gl, :, :, :, j],
-                        in1=tops[:, gl, :, j].unsqueeze(1).unsqueeze(1).to_broadcast([P, TAPS, TAPS, SIDE]),
-                        op=ALU.subtract,
-                    )
-                live = padded[:, gl].rearrange("p dy (j s) i -> p dy j (s i)", s=PITCH)[:, :, :, 0 : TAPS * SIDE]
-                nc.scalar.activation(out=live, in_=live, func=ACT.Exp)
-
-            for j in range(SIDE):
-                for dx in range(TAPS):
-                    u = j + dx - REACH
-                    if mirrored(u) != u:
-                        target = padded[:, :, :, PITCH * j + mirrored(u) - j + REACH, :]
-                        nc.vector.tensor_tensor(
-                            out=target, in0=target, in1=padded[:, :, :, PITCH * j + dx, :], op=ALU.add
-                        )
-
-            for i in range(SIDE):
-                skew = padded[:, :, :, REACH : REACH + SIDE * (PITCH - 1), i].rearrange(
-                    "p gl dy (j s) -> p j gl dy s", s=PITCH - 1
-                )[:, :, :, :, 0:SIDE]
-                first = max(0, REACH - i)
-                last = min(TAPS - 1, SIDE - 1 + REACH - i)
-                nc.vector.tensor_copy(
-                    out=shifted[i][:, :, :, first + i - REACH : last + i - REACH + 1, :],
-                    in_=skew[:, :, :, first : last + 1, :],
+                live = e[:, gl, 0 : TAPS * TAPS, :]
+                nc.vector.tensor_tensor(
+                    out=live,
+                    in0=lt[:, gl],
+                    in1=top[:, gl, 0:1, :].to_broadcast([P, TAPS * TAPS, SPOTS]),
+                    op=ALU.subtract,
                 )
+                nc.scalar.activation(out=live, in_=live, func=ACT.Exp)
+            taps = e[:, :, 0 : TAPS * TAPS, :].rearrange("p gl (dy dx) (i j) -> p gl dy dx i j", dx=TAPS, j=SIDE)
+            for i in range(SIDE):
                 for dy in range(TAPS):
                     u = i + dy - REACH
                     if mirrored(u) != u:
-                        row = shifted[i][:, :, :, mirrored(u), :]
-                        nc.vector.tensor_tensor(out=row, in0=row, in1=skew[:, :, :, dy, :], op=ALU.add)
+                        twin = taps[:, :, mirrored(u) - i + REACH, :, i, :]
+                        nc.vector.tensor_tensor(out=twin, in0=twin, in1=taps[:, :, dy, :, i, :], op=ALU.add)
+                        nc.gpsimd.memset(taps[:, :, dy, :, i, :], 0.0)
 
-        build_weights(0, 0)
-
-        bias_bf = keep.tile([P, 2, 8], BF16)
-        nc.sync.dma_start(out=bias_bf[:], in_=b3c.rearrange("(hh k c) -> k hh c", hh=2, k=P, c=8))
-        bias = keep.tile([P, 2, 8], F32)
+        bias_bf = keep.tile([P, 2, SHARE], BF16)
+        nc.sync.dma_start(out=bias_bf[:], in_=b3c.rearrange("(hh k c) -> k hh c", hh=2, k=P, c=SHARE))
+        bias = keep.tile([P, 2, SHARE], F32)
         nc.vector.tensor_copy(out=bias[:], in_=bias_bf[:])
 
-        codes_x = keep.tile([P, 1024], U32, align_bytes=64)
-        scales_x = keep.tile([P, 1024], U8, align_bytes=64)
-        x3 = keep.tile([P, 2, 256, 9], F32)
-        nc.vector.memset(x3[:, :, :, 8:9], 1.0)
+        raw_x = keep.tile([P, 32, 128], BF16)
+        nc.sync.dma_start(
+            out=raw_x[:],
+            in_=x.rearrange("b (g u p e) i j -> p (b g u) (e i j)", g=4, u=2, p=P, e=2),
+        )
+        grouped_x = keep.tile([P, 4, 4, SPOTS, 4], BF16, align_bytes=64)
+        raw_view = raw_x[:].rearrange("p (b g u) (e n) -> p g b n (u e)", b=4, g=4, u=2, e=2)
+        for g in range(4):
+            nc.vector.tensor_copy(out=grouped_x[:, g], in_=raw_view[:, g])
+        codes_x = keep.tile([P, 4, 256], U32, align_bytes=64)
+        scales_x = keep.tile([P, 4, 256], U8, align_bytes=64)
+        nc.vector.quantize_mx(
+            out=codes_x[:].rearrange("p g n -> p (g n)").bitcast(FP8X4),
+            scales=scales_x[:].rearrange("p g n -> p (g n)"),
+            in_=grouped_x[:].rearrange("p g b n f -> p (g b n f)"),
+        )
 
-        with tc.tile_pool(name="once", bufs=1) as once, tc.tile_pool(name="stream", bufs=2) as stream:
-            raw_x = once.tile([P, 32, 128], BF16)
-            nc.sync.dma_start(
-                out=raw_x[:],
-                in_=x.rearrange("b (g u p e) i j -> p (b g u) (e i j)", g=4, u=2, p=P, e=2),
-            )
-            grouped_x = once.tile([P, 2, 4, 2, 64, 4], BF16, align_bytes=64)
-            raw_view = raw_x[:].rearrange(
-                "p (t gl g u) (e n) -> p t g gl n (u e)", t=2, gl=2, g=4, u=2, e=2
-            )
-            for t in range(2):
-                nc.vector.tensor_copy(out=grouped_x[:, t], in_=raw_view[:, t])
-            nc.vector.quantize_mx(
-                out=codes_x[:].bitcast(FP8X4),
-                scales=scales_x[:],
-                in_=grouped_x[:].rearrange("p t g gl n f -> p (t g gl n f)"),
-            )
+        rows = [keep.tile([P, 4, SHARE, SIDE, WIDE], F32, name="rows%d" % hh) for hh in range(2)]
+        w_view = w3c.rearrange("(hh k c) q -> hh k c q", hh=2, k=P, c=SHARE)
 
-            for ot in range(8):
+        def project(hh):
+            for cp in range(SHARE // 2):
                 w_sb = stream.tile([P, 2, 2048], BF16)
-                nc.sync.dma_start(
-                    out=w_sb[:],
-                    in_=w3c[ot * 256 : (ot + 1) * 256, :].rearrange("(ob p) k -> p ob k", p=P),
-                )
+                nc.sync.dma_start(out=w_sb[:], in_=w_view[hh][:, 2 * cp : 2 * cp + 2, :])
                 grouped_w = stream.tile([P, 4, 256, 4], BF16, align_bytes=64)
                 for g in range(4):
-                    wt = psum.tile([P, 2, 256], F32, tag="turned", bufs=4)
+                    wt = psum.tile([P, 2, 256], F32, tag="proj")
                     for u in range(2):
-                        for ob in range(2):
-                            words = w_sb[:, ob, :].bitcast(F32)
+                        for cl in range(2):
+                            words = w_sb[:, cl, :].bitcast(F32)
                             nc.tensor.transpose(
-                                wt[:, u, ob * P : (ob + 1) * P],
+                                wt[:, u, cl * P : (cl + 1) * P],
                                 words[:, (2 * g + u) * P : (2 * g + u + 1) * P],
                                 ident[:],
                             )
@@ -155,85 +140,104 @@ def tile_sam_pb_kernel(tc, logits, x, w3c, b3c, out):
                     scales=scales_w[:].rearrange("p g o -> p (g o)"),
                     in_=grouped_w[:].rearrange("p g o f -> p (g o f)"),
                 )
-                acc = psum.tile([P, 2, 256], F32, tag="sums")
-                for t in range(2):
+                for cl in range(2):
+                    c = 2 * cp + cl
+                    x3 = psum.tile([P, 4, SIDE, SIDE], F32, tag="proj")
                     for g in range(4):
-                        cols = slice((t * 4 + g) * P, (t * 4 + g + 1) * P)
                         nc.tensor.matmul_mx(
-                            out=acc[:, t, :],
-                            lhsT=codes_x[:, cols].bitcast(FP8X4),
-                            lhsT_scale=scales_x[:, cols],
-                            rhs=codes_w[:, g, :].bitcast(FP8X4),
-                            rhs_scale=scales_w[:, g, :],
+                            out=x3[:].rearrange("p b i j -> p (b i j)"),
+                            lhsT=codes_w[:, g, cl * P : (cl + 1) * P].bitcast(FP8X4),
+                            lhsT_scale=scales_w[:, g, cl * P : (cl + 1) * P],
+                            rhs=codes_x[:, g, :].bitcast(FP8X4),
+                            rhs_scale=scales_x[:, g, :],
                             start=(g == 0),
                             stop=(g == 3),
                         )
-                nc.scalar.copy(
-                    out=x3[:, :, ot * 32 : (ot + 1) * 32, 0:8],
-                    in_=acc[:].rearrange("p t (h c) -> p t h c", c=8),
+                    nc.scalar.activation(
+                        out=rows[hh][:, :, c, :, REACH : REACH + SIDE],
+                        in_=x3[:],
+                        func=ACT.Identity,
+                        bias=bias[:, hh, c : c + 1],
+                    )
+                pair = rows[hh][:, :, 2 * cp : 2 * cp + 2]
+                for q in list(range(REACH)) + list(range(REACH + SIDE, WIDE)):
+                    nc.gpsimd.tensor_copy(
+                        out=pair[:, :, :, :, q], in_=pair[:, :, :, :, mirrored(q - REACH) + REACH]
+                    )
+
+        out_view = out.rearrange("b (hh k c) i j -> b hh k (c i j)", hh=2, k=P, c=SHARE)
+
+        def window_sum(hh, t, gl, e):
+            both = psum.tile([P, P], F32, tag="aux")
+            for pair in range((TAPS * TAPS + 1) // 2):
+                nc.tensor.matmul(
+                    out=both[:],
+                    lhsT=e[:, gl, 2 * pair : 2 * pair + 2, :].rearrange("p l n -> p (l n)"),
+                    rhs=ident[:],
+                    is_transpose=True,
+                    start=(pair == 0),
+                    stop=(pair == (TAPS * TAPS - 1) // 2),
                 )
+            turned = ends.tile([P, 5, P], F32)
+            nc.scalar.copy(out=turned[:, 4, :], in_=both[:])
 
-        wide = stack.enter_context(tc.tile_pool(name="wide", bufs=1))
-        window = wide.tile([P, P, P], F32)
-        nc.vector.memset(window[0:64, :, 64:128], 0.0)
-        nc.gpsimd.memset(window[64:128, :, 0:64], 0.0)
-
-        out_view = out.rearrange("b (hh k c) i j -> b hh k (c i j)", hh=2, k=P, c=8)
-        chunks = [(hh, t) for hh in range(2) for t in range(2)]
-        for index, (hh, t) in enumerate(chunks):
-            for i in range(SIDE):
-                for jh in range(2):
-                    turned = psum.tile([P, 4, P], F32, tag="turned", bufs=4)
-                    for s in range(4):
-                        nc.tensor.transpose(
-                            turned[:, s, :],
-                            shifted[i][:, 4 * jh + s].rearrange("p gl mi mj -> p (gl mi mj)"),
-                            ident[:],
+            taps = e[:, gl, 0 : TAPS * TAPS, :].rearrange("p (dy dx) (i j) -> p dy dx i j", dx=TAPS, j=SIDE)
+            sums = [psum.tile([P, P], F32, tag="acc", bufs=4, name="sums%d" % q) for q in range(4)]
+            for dx in range(TAPS):
+                for dy in range(TAPS):
+                    first = max(0, REACH - dy)
+                    last = min(SIDE - 1, SIDE - 1 + REACH - dy)
+                    product = products[dy][dx % 2]
+                    nc.vector.tensor_tensor(
+                        out=product[:, :, first : last + 1, :],
+                        in0=rows[hh][:, 2 * t + gl, :, first + dy - REACH : last + dy - REACH + 1, dx : dx + SIDE],
+                        in1=taps[:, dy, dx, first : last + 1, :]
+                        .unsqueeze(1)
+                        .to_broadcast([P, SHARE, last + 1 - first, SIDE]),
+                        op=ALU.mult,
+                    )
+                    for q in range(4):
+                        nc.tensor.matmul(
+                            out=sums[q][:],
+                            lhsT=product[:, 2 * q : 2 * q + 2].rearrange("p c i j -> p (c i j)"),
+                            rhs=ident[:],
+                            is_transpose=True,
+                            start=(dx == 0 and dy == 0),
+                            stop=(dx == TAPS - 1 and dy == TAPS - 1),
                         )
-                    n0 = SIDE * i + 4 * jh
-                    nc.vector.tensor_copy(
-                        out=window[0:64, :, n0 : n0 + 4], in_=turned[0:64].rearrange("p s k -> p k s")
-                    )
-                    nc.scalar.copy(
-                        out=window[64:128, :, 64 + n0 : 64 + n0 + 4],
-                        in_=turned[64:128].rearrange("p s k -> p k s"),
-                    )
-            if index + 1 < len(chunks):
-                build_weights(*chunks[index + 1])
+            for q in range(4):
+                nc.scalar.copy(out=turned[:, q, :], in_=sums[q][:])
 
-            normed = ends.tile([P, 8, P], F32)
-            for kb in range(4):
-                sums = psum.tile([P, 32, 9], F32, tag="sums")
-                for kk in range(32):
-                    k = kb * 32 + kk
-                    nc.tensor.matmul(
-                        out=sums[:, kk, :],
-                        lhsT=window[:, k, :],
-                        rhs=x3[:, t, hh * P + k, :],
-                        start=True,
-                        stop=True,
-                    )
-                rec = ends.tile([P, 32, 1], F32)
-                nc.vector.reciprocal(out=rec[:], in_=sums[:, :, 8:9])
-                nc.vector.tensor_tensor(
-                    out=normed[:, :, kb * 32 : (kb + 1) * 32],
-                    in0=sums[:, :, 0:8].rearrange("p k c -> p c k"),
-                    in1=rec[:].rearrange("p k o -> p o k").to_broadcast([P, 8, 32]),
-                    op=ALU.mult,
+            back = psum.tile([P, SHARE, SPOTS], F32, tag="aux")
+            for q in range(4):
+                nc.tensor.transpose(
+                    back[:, 2 * q : 2 * q + 2, :].rearrange("p c n -> p (c n)"), turned[:, q, :], ident[:]
                 )
-            result = ends.tile([P, 2, 8, 64], F32)
-            for half in range(2):
-                flipped = psum.tile([P, 4, P], F32, tag="flipped")
-                for cc in range(4):
-                    nc.tensor.transpose(flipped[:, cc, :], normed[:, half * 4 + cc, :], ident[:])
-                nc.vector.tensor_tensor(
-                    out=result[:, :, half * 4 : (half + 1) * 4, :].rearrange("p gl c n -> p c gl n"),
-                    in0=flipped[:].rearrange("p c (gl n) -> p c gl n", gl=2),
-                    in1=bias[:, hh, half * 4 : (half + 1) * 4]
-                    .unsqueeze(2)
-                    .unsqueeze(3)
-                    .to_broadcast([P, 4, 2, 64]),
-                    op=ALU.add,
-                )
-            for gl in range(2):
-                nc.sync.dma_start(out=out_view[2 * t + gl, hh], in_=result[:, gl].rearrange("p c n -> p (c n)"))
+            total = psum.tile([P, P], F32, tag="aux")
+            nc.tensor.matmul(
+                out=total[:], lhsT=turned[:, 4, :], rhs=ident[:], is_transpose=True, start=True, stop=False
+            )
+            nc.tensor.matmul(
+                out=total[:], lhsT=turned[:, 4, :], rhs=exchange[:], is_transpose=True, start=False, stop=True
+            )
+            rec = ends.tile([P, SPOTS], F32)
+            nc.vector.reciprocal(out=rec[:], in_=total[:, 0:SPOTS])
+            result = ends.tile([P, SHARE, SPOTS], F32)
+            nc.vector.tensor_tensor(
+                out=result[:],
+                in0=back[:],
+                in1=rec[:].unsqueeze(1).to_broadcast([P, SHARE, SPOTS]),
+                op=ALU.mult,
+            )
+            nc.sync.dma_start(out=out_view[2 * t + gl, hh], in_=result[:].rearrange("p c n -> p (c n)"))
+
+        chunks = [(hh, t) for hh in range(2) for t in range(2)]
+        softmax_numerators(0, 0, weights[0])
+        project(0)
+        for index, (hh, t) in enumerate(chunks):
+            window_sum(hh, t, 0, weights[index % 2])
+            if index + 1 < len(chunks):
+                softmax_numerators(*chunks[index + 1], weights[(index + 1) % 2])
+            if index == 0:
+                project(1)
+            window_sum(hh, t, 1, weights[index % 2])

@@ -48,14 +48,14 @@ def tile_sam_pb_kernel(tc, logits, x, w3c, b3c, out):
         for r in range(2):
             nc.vector.memset(weights[r][:, :, TAPS * TAPS :, :], 0.0)
         products = [
-            [keep.tile([P, SHARE, SIDE, SIDE], F32, name="products%d_%d" % (dy, r)) for r in range(2)]
+            [keep.tile([P, SIDE, SHARE, SIDE], F32, name="products%d_%d" % (dy, r)) for r in range(2)]
             for dy in range(TAPS)
         ]
         for dy in range(TAPS):
             for r in range(2):
                 nc.vector.memset(products[dy][r][:], 0.0)
 
-        def softmax_numerators(hh, t, e):
+        def shifted_exponentials(hh, t, e):
             lt = loads.tile([P, 2, TAPS * TAPS, SPOTS], BF16)
             for gl in range(2):
                 nc.sync.dma_start(out=lt[:, gl], in_=logits[2 * t + gl, hh * P : (hh + 1) * P])
@@ -83,6 +83,8 @@ def tile_sam_pb_kernel(tc, logits, x, w3c, b3c, out):
                     op=ALU.subtract,
                 )
                 nc.scalar.activation(out=live, in_=live, func=ACT.Exp)
+
+        def fold_mirrored_rows(e):
             taps = e[:, :, 0 : TAPS * TAPS, :].rearrange("p gl (dy dx) (i j) -> p gl dy dx i j", dx=TAPS, j=SIDE)
             for i in range(SIDE):
                 for dy in range(TAPS):
@@ -117,8 +119,8 @@ def tile_sam_pb_kernel(tc, logits, x, w3c, b3c, out):
         rows = [keep.tile([P, 4, SHARE, SIDE, WIDE], F32, name="rows%d" % hh) for hh in range(2)]
         w_view = w3c.rearrange("(hh k c) q -> hh k c q", hh=2, k=P, c=SHARE)
 
-        def project(hh):
-            for cp in range(SHARE // 2):
+        def project(hh, pairs):
+            for cp in pairs:
                 w_sb = stream.tile([P, 2, 2048], BF16)
                 nc.sync.dma_start(out=w_sb[:], in_=w_view[hh][:, 2 * cp : 2 * cp + 2, :])
                 grouped_w = stream.tile([P, 4, 256, 4], BF16, align_bytes=64)
@@ -165,6 +167,10 @@ def tile_sam_pb_kernel(tc, logits, x, w3c, b3c, out):
                         out=pair[:, :, :, :, q], in_=pair[:, :, :, :, mirrored(q - REACH) + REACH]
                     )
 
+        reaching = [
+            [dy for dy in range(TAPS) if max(0, REACH - dy) <= 2 * q + 1 and min(SIDE - 1, SIDE - 1 + REACH - dy) >= 2 * q]
+            for q in range(4)
+        ]
         out_view = out.rearrange("b (hh k c) i j -> b hh k (c i j)", hh=2, k=P, c=SHARE)
 
         def window_sum(hh, t, gl, e):
@@ -189,29 +195,32 @@ def tile_sam_pb_kernel(tc, logits, x, w3c, b3c, out):
                     last = min(SIDE - 1, SIDE - 1 + REACH - dy)
                     product = products[dy][dx % 2]
                     nc.vector.tensor_tensor(
-                        out=product[:, :, first : last + 1, :],
-                        in0=rows[hh][:, 2 * t + gl, :, first + dy - REACH : last + dy - REACH + 1, dx : dx + SIDE],
+                        out=product[:, first : last + 1, :, :],
+                        in0=rows[hh][
+                            :, 2 * t + gl, :, first + dy - REACH : last + dy - REACH + 1, dx : dx + SIDE
+                        ].rearrange("p c i j -> p i c j"),
                         in1=taps[:, dy, dx, first : last + 1, :]
-                        .unsqueeze(1)
-                        .to_broadcast([P, SHARE, last + 1 - first, SIDE]),
+                        .unsqueeze(2)
+                        .to_broadcast([P, last + 1 - first, SHARE, SIDE]),
                         op=ALU.mult,
                     )
                     for q in range(4):
-                        nc.tensor.matmul(
-                            out=sums[q][:],
-                            lhsT=product[:, 2 * q : 2 * q + 2].rearrange("p c i j -> p (c i j)"),
-                            rhs=ident[:],
-                            is_transpose=True,
-                            start=(dx == 0 and dy == 0),
-                            stop=(dx == TAPS - 1 and dy == TAPS - 1),
-                        )
+                        if dy in reaching[q]:
+                            nc.tensor.matmul(
+                                out=sums[q][:],
+                                lhsT=product[:, 2 * q : 2 * q + 2].rearrange("p i c j -> p (i c j)"),
+                                rhs=ident[:],
+                                is_transpose=True,
+                                start=(dx == 0 and dy == reaching[q][0]),
+                                stop=(dx == TAPS - 1 and dy == reaching[q][-1]),
+                            )
             for q in range(4):
                 nc.scalar.copy(out=turned[:, q, :], in_=sums[q][:])
 
-            back = psum.tile([P, SHARE, SPOTS], F32, tag="aux")
+            back = psum.tile([P, SIDE, SHARE, SIDE], F32, tag="aux")
             for q in range(4):
                 nc.tensor.transpose(
-                    back[:, 2 * q : 2 * q + 2, :].rearrange("p c n -> p (c n)"), turned[:, q, :], ident[:]
+                    back[:, 2 * q : 2 * q + 2].rearrange("p i c j -> p (i c j)"), turned[:, q, :], ident[:]
                 )
             total = psum.tile([P, P], F32, tag="aux")
             nc.tensor.matmul(
@@ -222,22 +231,31 @@ def tile_sam_pb_kernel(tc, logits, x, w3c, b3c, out):
             )
             rec = ends.tile([P, SPOTS], F32)
             nc.vector.reciprocal(out=rec[:], in_=total[:, 0:SPOTS])
-            result = ends.tile([P, SHARE, SPOTS], F32)
+            result = ends.tile([P, SHARE, SIDE, SIDE], F32)
             nc.vector.tensor_tensor(
                 out=result[:],
-                in0=back[:],
-                in1=rec[:].unsqueeze(1).to_broadcast([P, SHARE, SPOTS]),
+                in0=back[:].rearrange("p i c j -> p c i j"),
+                in1=rec[:]
+                .rearrange("p (i j) -> p i j", j=SIDE)
+                .unsqueeze(1)
+                .to_broadcast([P, SHARE, SIDE, SIDE]),
                 op=ALU.mult,
             )
-            nc.sync.dma_start(out=out_view[2 * t + gl, hh], in_=result[:].rearrange("p c n -> p (c n)"))
+            nc.sync.dma_start(out=out_view[2 * t + gl, hh], in_=result[:].rearrange("p c i j -> p (c i j)"))
 
         chunks = [(hh, t) for hh in range(2) for t in range(2)]
-        softmax_numerators(0, 0, weights[0])
-        project(0)
+        shifted_exponentials(*chunks[0], weights[0])
+        project(0, range(0, 2))
+        shifted_exponentials(*chunks[1], weights[1])
+        project(0, range(2, 4))
+        fold_mirrored_rows(weights[0])
+        fold_mirrored_rows(weights[1])
         for index, (hh, t) in enumerate(chunks):
             window_sum(hh, t, 0, weights[index % 2])
-            if index + 1 < len(chunks):
-                softmax_numerators(*chunks[index + 1], weights[(index + 1) % 2])
             if index == 0:
-                project(1)
+                project(1, range(0, 4))
+            elif index + 1 < len(chunks):
+                fold_mirrored_rows(weights[(index + 1) % 2])
             window_sum(hh, t, 1, weights[index % 2])
+            if index + 2 < len(chunks):
+                shifted_exponentials(*chunks[index + 2], weights[index % 2])

@@ -41,19 +41,19 @@ def tile_sam_pb_kernel(tc, logits, x, w3c, b3c, out):
         ident = keep.tile([P, P], F32)
         make_identity(nc, ident[:])
         exchange = keep.tile([P, P], F32)
-        nc.vector.tensor_copy(out=exchange[:, 0:SPOTS], in_=ident[:, SPOTS:P])
-        nc.vector.tensor_copy(out=exchange[:, SPOTS:P], in_=ident[:, 0:SPOTS])
+        nc.scalar.copy(out=exchange[:, 0:SPOTS], in_=ident[:, SPOTS:P])
+        nc.scalar.copy(out=exchange[:, SPOTS:P], in_=ident[:, 0:SPOTS])
 
         weights = [keep.tile([P, 2, TAPS * TAPS + 1, SPOTS], F32, name="weights%d" % r) for r in range(2)]
         for r in range(2):
-            nc.vector.memset(weights[r][:, :, TAPS * TAPS :, :], 0.0)
+            nc.gpsimd.memset(weights[r][:, :, TAPS * TAPS :, :], 0.0)
         products = [
             [keep.tile([P, SIDE, SHARE, SIDE], F32, name="products%d_%d" % (dy, r)) for r in range(2)]
             for dy in range(TAPS)
         ]
         for dy in range(TAPS):
             for r in range(2):
-                nc.vector.memset(products[dy][r][:], 0.0)
+                nc.gpsimd.memset(products[dy][r][:], 0.0)
 
         def shifted_exponentials(hh, t, e):
             lt = loads.tile([P, 2, TAPS * TAPS, SPOTS], BF16)
@@ -97,7 +97,7 @@ def tile_sam_pb_kernel(tc, logits, x, w3c, b3c, out):
         bias_bf = keep.tile([P, 2, SHARE], BF16)
         nc.sync.dma_start(out=bias_bf[:], in_=b3c.rearrange("(hh k c) -> k hh c", hh=2, k=P, c=SHARE))
         bias = keep.tile([P, 2, SHARE], F32)
-        nc.vector.tensor_copy(out=bias[:], in_=bias_bf[:])
+        nc.scalar.copy(out=bias[:], in_=bias_bf[:])
 
         raw_x = keep.tile([P, 32, 128], BF16)
         nc.sync.dma_start(
@@ -107,7 +107,7 @@ def tile_sam_pb_kernel(tc, logits, x, w3c, b3c, out):
         grouped_x = keep.tile([P, 4, 4, SPOTS, 4], BF16, align_bytes=64)
         raw_view = raw_x[:].rearrange("p (b g u) (e n) -> p g b n (u e)", b=4, g=4, u=2, e=2)
         for g in range(4):
-            nc.vector.tensor_copy(out=grouped_x[:, g], in_=raw_view[:, g])
+            nc.scalar.copy(out=grouped_x[:, g], in_=raw_view[:, g])
         codes_x = keep.tile([P, 4, 256], U32, align_bytes=64)
         scales_x = keep.tile([P, 4, 256], U8, align_bytes=64)
         nc.vector.quantize_mx(
@@ -167,67 +167,40 @@ def tile_sam_pb_kernel(tc, logits, x, w3c, b3c, out):
                         out=pair[:, :, :, :, q], in_=pair[:, :, :, :, mirrored(q - REACH) + REACH]
                     )
 
-        reaching = [
-            [dy for dy in range(TAPS) if max(0, REACH - dy) <= 2 * q + 1 and min(SIDE - 1, SIDE - 1 + REACH - dy) >= 2 * q]
-            for q in range(4)
-        ]
         out_view = out.rearrange("b (hh k c) i j -> b hh k (c i j)", hh=2, k=P, c=SHARE)
 
-        def window_sum(hh, t, gl, e):
-            both = psum.tile([P, P], F32, tag="aux")
-            for pair in range((TAPS * TAPS + 1) // 2):
-                nc.tensor.matmul(
-                    out=both[:],
-                    lhsT=e[:, gl, 2 * pair : 2 * pair + 2, :].rearrange("p l n -> p (l n)"),
-                    rhs=ident[:],
-                    is_transpose=True,
-                    start=(pair == 0),
-                    stop=(pair == (TAPS * TAPS - 1) // 2),
-                )
-            turned = ends.tile([P, 5, P], F32)
-            nc.scalar.copy(out=turned[:, 4, :], in_=both[:])
-
-            taps = e[:, gl, 0 : TAPS * TAPS, :].rearrange("p (dy dx) (i j) -> p dy dx i j", dx=TAPS, j=SIDE)
-            sums = [psum.tile([P, P], F32, tag="acc", bufs=4, name="sums%d" % q) for q in range(4)]
-            for dx in range(TAPS):
-                for dy in range(TAPS):
-                    first = max(0, REACH - dy)
-                    last = min(SIDE - 1, SIDE - 1 + REACH - dy)
-                    product = products[dy][dx % 2]
-                    nc.vector.tensor_tensor(
-                        out=product[:, first : last + 1, :, :],
-                        in0=rows[hh][
-                            :, 2 * t + gl, :, first + dy - REACH : last + dy - REACH + 1, dx : dx + SIDE
-                        ].rearrange("p c i j -> p i c j"),
-                        in1=taps[:, dy, dx, first : last + 1, :]
-                        .unsqueeze(2)
-                        .to_broadcast([P, last + 1 - first, SHARE, SIDE]),
-                        op=ALU.mult,
+        def numerator_sums(e):
+            turned_sums = []
+            for gl in range(2):
+                both = psum.tile([P, P], F32, tag="aux", bufs=4)
+                for pair in range((TAPS * TAPS + 1) // 2):
+                    nc.tensor.matmul(
+                        out=both[:],
+                        lhsT=e[:, gl, 2 * pair : 2 * pair + 2, :].rearrange("p l n -> p (l n)"),
+                        rhs=ident[:],
+                        is_transpose=True,
+                        start=(pair == 0),
+                        stop=(pair == (TAPS * TAPS - 1) // 2),
                     )
-                    for q in range(4):
-                        if dy in reaching[q]:
-                            nc.tensor.matmul(
-                                out=sums[q][:],
-                                lhsT=product[:, 2 * q : 2 * q + 2].rearrange("p i c j -> p (i c j)"),
-                                rhs=ident[:],
-                                is_transpose=True,
-                                start=(dx == 0 and dy == reaching[q][0]),
-                                stop=(dx == TAPS - 1 and dy == reaching[q][-1]),
-                            )
-            for q in range(4):
-                nc.scalar.copy(out=turned[:, q, :], in_=sums[q][:])
+                turned_sum = ends.tile([P, P], F32, bufs=6)
+                nc.scalar.copy(out=turned_sum[:], in_=both[:])
+                turned_sums.append(turned_sum)
+            return turned_sums
 
-            back = psum.tile([P, SIDE, SHARE, SIDE], F32, tag="aux")
+        def finish(hh, t, gl, sums, turned_sum):
+            turned = ends.tile([P, 4, P], F32)
+            nc.scalar.copy(out=turned[:], in_=sums[:])
+            back = psum.tile([P, SIDE, SHARE, SIDE], F32, tag="aux", bufs=4)
             for q in range(4):
                 nc.tensor.transpose(
                     back[:, 2 * q : 2 * q + 2].rearrange("p i c j -> p (i c j)"), turned[:, q, :], ident[:]
                 )
-            total = psum.tile([P, P], F32, tag="aux")
+            total = psum.tile([P, P], F32, tag="aux", bufs=4)
             nc.tensor.matmul(
-                out=total[:], lhsT=turned[:, 4, :], rhs=ident[:], is_transpose=True, start=True, stop=False
+                out=total[:], lhsT=turned_sum[:], rhs=ident[:], is_transpose=True, start=True, stop=False
             )
             nc.tensor.matmul(
-                out=total[:], lhsT=turned[:, 4, :], rhs=exchange[:], is_transpose=True, start=False, stop=True
+                out=total[:], lhsT=turned_sum[:], rhs=exchange[:], is_transpose=True, start=False, stop=True
             )
             rec = ends.tile([P, SPOTS], F32)
             nc.vector.reciprocal(out=rec[:], in_=total[:, 0:SPOTS])
@@ -243,6 +216,38 @@ def tile_sam_pb_kernel(tc, logits, x, w3c, b3c, out):
             )
             nc.sync.dma_start(out=out_view[2 * t + gl, hh], in_=result[:].rearrange("p c i j -> p (c i j)"))
 
+        def window_sum(hh, t, gl, e, waiting):
+            taps = e[:, gl, 0 : TAPS * TAPS, :].rearrange("p (dy dx) (i j) -> p dy dx i j", dx=TAPS, j=SIDE)
+            sums = psum.tile([P, 4, P], F32, tag="acc")
+            for dx in range(TAPS):
+                for dy in range(TAPS):
+                    first = max(0, REACH - dy)
+                    last = min(SIDE - 1, SIDE - 1 + REACH - dy)
+                    product = products[dy][dx % 2]
+                    nc.vector.tensor_tensor(
+                        out=product[:, first : last + 1, :, :],
+                        in0=rows[hh][
+                            :, 2 * t + gl, :, first + dy - REACH : last + dy - REACH + 1, dx : dx + SIDE
+                        ].rearrange("p c i j -> p i c j"),
+                        in1=taps[:, dy, dx, first : last + 1, :]
+                        .unsqueeze(2)
+                        .to_broadcast([P, last + 1 - first, SHARE, SIDE]),
+                        op=ALU.mult,
+                    )
+                    pieces = range(first // 2, last // 2 + 1)
+                    for q in pieces:
+                        nc.tensor.matmul(
+                            out=sums[:, q, :],
+                            lhsT=product[:, 2 * q : 2 * q + 2].rearrange("p i c j -> p (i c j)"),
+                            rhs=ident[:],
+                            is_transpose=True,
+                            start=(dx == 0 and dy == 0 and q == pieces[0]),
+                            stop=(dx == TAPS - 1 and dy == TAPS - 1 and q == pieces[-1]),
+                        )
+                if dx == 0 and waiting:
+                    finish(*waiting)
+            return sums
+
         chunks = [(hh, t) for hh in range(2) for t in range(2)]
         shifted_exponentials(*chunks[0], weights[0])
         project(0, range(0, 2))
@@ -250,12 +255,18 @@ def tile_sam_pb_kernel(tc, logits, x, w3c, b3c, out):
         project(0, range(2, 4))
         fold_mirrored_rows(weights[0])
         fold_mirrored_rows(weights[1])
+        turned_sums = [numerator_sums(weights[0]), numerator_sums(weights[1])]
+        waiting = None
         for index, (hh, t) in enumerate(chunks):
-            window_sum(hh, t, 0, weights[index % 2])
+            e = weights[index % 2]
+            sums = window_sum(hh, t, 0, e, waiting)
+            waiting = (hh, t, 0, sums, turned_sums[index % 2][0])
             if index == 0:
                 project(1, range(0, 4))
-            elif index + 1 < len(chunks):
-                fold_mirrored_rows(weights[(index + 1) % 2])
-            window_sum(hh, t, 1, weights[index % 2])
+            sums = window_sum(hh, t, 1, e, waiting)
+            waiting = (hh, t, 1, sums, turned_sums[index % 2][1])
             if index + 2 < len(chunks):
-                shifted_exponentials(*chunks[index + 2], weights[index % 2])
+                shifted_exponentials(*chunks[index + 2], e)
+                fold_mirrored_rows(e)
+                turned_sums[index % 2] = numerator_sums(e)
+        finish(*waiting)

@@ -172,7 +172,7 @@ def tile_sam_pb_kernel(tc, logits, x, w3c, b3c, out):
         def numerator_sums(e):
             turned_sums = []
             for gl in range(2):
-                both = psum.tile([P, P], F32, tag="aux", bufs=4)
+                both = psum.tile([P, P], F32, tag="aux")
                 for pair in range((TAPS * TAPS + 1) // 2):
                     nc.tensor.matmul(
                         out=both[:],
@@ -189,13 +189,16 @@ def tile_sam_pb_kernel(tc, logits, x, w3c, b3c, out):
 
         def finish(hh, t, gl, sums, turned_sum):
             turned = ends.tile([P, 4, P], F32)
-            nc.scalar.copy(out=turned[:], in_=sums[:])
-            back = psum.tile([P, SIDE, SHARE, SIDE], F32, tag="aux", bufs=4)
+            for bank in range(2):
+                nc.scalar.copy(
+                    out=turned[:].rearrange("p (h bank) k -> p bank h k", bank=2)[:, bank], in_=sums[bank][:]
+                )
+            back = psum.tile([P, SIDE, SHARE, SIDE], F32, tag="aux")
             for q in range(4):
                 nc.tensor.transpose(
                     back[:, 2 * q : 2 * q + 2].rearrange("p i c j -> p (i c j)"), turned[:, q, :], ident[:]
                 )
-            total = psum.tile([P, P], F32, tag="aux", bufs=4)
+            total = psum.tile([P, P], F32, tag="aux")
             nc.tensor.matmul(
                 out=total[:], lhsT=turned_sum[:], rhs=ident[:], is_transpose=True, start=True, stop=False
             )
@@ -218,7 +221,7 @@ def tile_sam_pb_kernel(tc, logits, x, w3c, b3c, out):
 
         def window_sum(hh, t, gl, e, waiting):
             taps = e[:, gl, 0 : TAPS * TAPS, :].rearrange("p (dy dx) (i j) -> p dy dx i j", dx=TAPS, j=SIDE)
-            sums = psum.tile([P, 4, P], F32, tag="acc")
+            sums = [psum.tile([P, 2, P], F32, tag="acc", bufs=4, name="sums%d" % bank) for bank in range(2)]
             for dx in range(TAPS):
                 for dy in range(TAPS):
                     first = max(0, REACH - dy)
@@ -237,12 +240,12 @@ def tile_sam_pb_kernel(tc, logits, x, w3c, b3c, out):
                     pieces = range(first // 2, last // 2 + 1)
                     for q in pieces:
                         nc.tensor.matmul(
-                            out=sums[:, q, :],
+                            out=sums[q % 2][:, q // 2, :],
                             lhsT=product[:, 2 * q : 2 * q + 2].rearrange("p i c j -> p (i c j)"),
                             rhs=ident[:],
                             is_transpose=True,
-                            start=(dx == 0 and dy == 0 and q == pieces[0]),
-                            stop=(dx == TAPS - 1 and dy == TAPS - 1 and q == pieces[-1]),
+                            start=(dx == 0 and dy == 0 and q in pieces[:2]),
+                            stop=(dx == TAPS - 1 and dy == TAPS - 1 and q in pieces[-2:]),
                         )
                 if dx == 0 and waiting:
                     finish(*waiting)

@@ -18,6 +18,7 @@ TAPS = 7
 REACH = TAPS // 2
 WIDE = SIDE + 2 * REACH
 SHARE = 8
+DEPTH = 7
 FLOPS = 2 * 2048 * 2048 * 256 + 2 * 4 * 2048 * 64 * 49
 
 
@@ -40,20 +41,8 @@ def tile_sam_pb_kernel(tc, logits, x, w3c, b3c, out):
 
         ident = keep.tile([P, P], F32)
         make_identity(nc, ident[:])
-        exchange = keep.tile([P, P], F32)
-        nc.scalar.copy(out=exchange[:, 0:SPOTS], in_=ident[:, SPOTS:P])
-        nc.scalar.copy(out=exchange[:, SPOTS:P], in_=ident[:, 0:SPOTS])
 
-        weights = [keep.tile([P, 2, TAPS * TAPS + 1, SPOTS], F32, name="weights%d" % r) for r in range(2)]
-        for r in range(2):
-            nc.gpsimd.memset(weights[r][:, :, TAPS * TAPS :, :], 0.0)
-        products = [
-            [keep.tile([P, SIDE, SHARE, SIDE], F32, name="products%d_%d" % (dy, r)) for r in range(2)]
-            for dy in range(TAPS)
-        ]
-        for dy in range(TAPS):
-            for r in range(2):
-                nc.gpsimd.memset(products[dy][r][:], 0.0)
+        weights = [keep.tile([P, TAPS * TAPS, SIDE, 2, SIDE], F32, name="weights%d" % r) for r in range(2)]
 
         def shifted_exponentials(hh, t, e):
             lt = loads.tile([P, 2, TAPS * TAPS, SPOTS], BF16)
@@ -75,24 +64,26 @@ def tile_sam_pb_kernel(tc, logits, x, w3c, b3c, out):
                 out=top[:, :, 0:1, :], in0=top[:, :, 0:1, :], in1=lt[:, :, 48:49, :], op=ALU.max
             )
             for gl in range(2):
-                live = e[:, gl, 0 : TAPS * TAPS, :]
                 nc.vector.tensor_tensor(
-                    out=live,
-                    in0=lt[:, gl],
-                    in1=top[:, gl, 0:1, :].to_broadcast([P, TAPS * TAPS, SPOTS]),
+                    out=e[:, :, :, gl, :],
+                    in0=lt[:, gl].rearrange("p l (i j) -> p l i j", j=SIDE),
+                    in1=top[:, gl, 0:1, :]
+                    .rearrange("p l (i j) -> p l i j", j=SIDE)
+                    .to_broadcast([P, TAPS * TAPS, SIDE, SIDE]),
                     op=ALU.subtract,
                 )
-                nc.scalar.activation(out=live, in_=live, func=ACT.Exp)
+            flat = e[:].rearrange("p l i gl j -> p (l i gl j)")
+            nc.scalar.activation(out=flat, in_=flat, func=ACT.Exp)
 
         def fold_mirrored_rows(e):
-            taps = e[:, :, 0 : TAPS * TAPS, :].rearrange("p gl (dy dx) (i j) -> p gl dy dx i j", dx=TAPS, j=SIDE)
+            taps = e[:].rearrange("p (dy dx) i gl j -> p dy dx i (gl j)", dx=TAPS)
             for i in range(SIDE):
                 for dy in range(TAPS):
                     u = i + dy - REACH
                     if mirrored(u) != u:
-                        twin = taps[:, :, mirrored(u) - i + REACH, :, i, :]
-                        nc.vector.tensor_tensor(out=twin, in0=twin, in1=taps[:, :, dy, :, i, :], op=ALU.add)
-                        nc.gpsimd.memset(taps[:, :, dy, :, i, :], 0.0)
+                        twin = taps[:, mirrored(u) - i + REACH, :, i, :]
+                        nc.vector.tensor_tensor(out=twin, in0=twin, in1=taps[:, dy, :, i, :], op=ALU.add)
+                        nc.gpsimd.memset(taps[:, dy, :, i, :], 0.0)
 
         bias_bf = keep.tile([P, 2, SHARE], BF16)
         nc.sync.dma_start(out=bias_bf[:], in_=b3c.rearrange("(hh k c) -> k hh c", hh=2, k=P, c=SHARE))
@@ -170,82 +161,76 @@ def tile_sam_pb_kernel(tc, logits, x, w3c, b3c, out):
         out_view = out.rearrange("b (hh k c) i j -> b hh k (c i j)", hh=2, k=P, c=SHARE)
 
         def numerator_sums(e):
-            turned_sums = []
-            for gl in range(2):
-                both = psum.tile([P, P], F32, tag="aux")
-                for pair in range((TAPS * TAPS + 1) // 2):
-                    nc.tensor.matmul(
-                        out=both[:],
-                        lhsT=e[:, gl, 2 * pair : 2 * pair + 2, :].rearrange("p l n -> p (l n)"),
-                        rhs=ident[:],
-                        is_transpose=True,
-                        start=(pair == 0),
-                        stop=(pair == (TAPS * TAPS - 1) // 2),
-                    )
-                turned_sum = ends.tile([P, P], F32, bufs=6)
-                nc.scalar.copy(out=turned_sum[:], in_=both[:])
-                turned_sums.append(turned_sum)
-            return turned_sums
+            both = psum.tile([P, P], F32, tag="aux")
+            for tap in range(TAPS * TAPS):
+                nc.tensor.matmul(
+                    out=both[:],
+                    lhsT=e[:, tap].rearrange("p i gl j -> p (i gl j)"),
+                    rhs=ident[:],
+                    is_transpose=True,
+                    start=(tap == 0),
+                    stop=(tap == TAPS * TAPS - 1),
+                )
+            turned_sum = ends.tile([P, P], F32, bufs=3)
+            nc.scalar.copy(out=turned_sum[:], in_=both[:])
+            return turned_sum
 
-        def finish(hh, t, gl, sums, turned_sum):
-            turned = ends.tile([P, 4, P], F32)
+        def finish(hh, t, sums, turned_sum):
+            turned = ends.tile([P, SIDE, P], F32)
             for bank in range(2):
                 nc.scalar.copy(
                     out=turned[:].rearrange("p (h bank) k -> p bank h k", bank=2)[:, bank], in_=sums[bank][:]
                 )
-            back = psum.tile([P, SIDE, SHARE, SIDE], F32, tag="aux")
-            for q in range(4):
-                nc.tensor.transpose(
-                    back[:, 2 * q : 2 * q + 2].rearrange("p i c j -> p (i c j)"), turned[:, q, :], ident[:]
-                )
-            total = psum.tile([P, P], F32, tag="aux")
-            nc.tensor.matmul(
-                out=total[:], lhsT=turned_sum[:], rhs=ident[:], is_transpose=True, start=True, stop=False
-            )
-            nc.tensor.matmul(
-                out=total[:], lhsT=turned_sum[:], rhs=exchange[:], is_transpose=True, start=False, stop=True
-            )
-            rec = ends.tile([P, SPOTS], F32)
-            nc.vector.reciprocal(out=rec[:], in_=total[:, 0:SPOTS])
-            result = ends.tile([P, SHARE, SIDE, SIDE], F32)
-            nc.vector.tensor_tensor(
-                out=result[:],
-                in0=back[:].rearrange("p i c j -> p c i j"),
-                in1=rec[:]
-                .rearrange("p (i j) -> p i j", j=SIDE)
-                .unsqueeze(1)
-                .to_broadcast([P, SHARE, SIDE, SIDE]),
-                op=ALU.mult,
-            )
-            nc.sync.dma_start(out=out_view[2 * t + gl, hh], in_=result[:].rearrange("p c i j -> p (c i j)"))
-
-        def window_sum(hh, t, gl, e, waiting):
-            taps = e[:, gl, 0 : TAPS * TAPS, :].rearrange("p (dy dx) (i j) -> p dy dx i j", dx=TAPS, j=SIDE)
-            sums = [psum.tile([P, 2, P], F32, tag="acc", bufs=4, name="sums%d" % bank) for bank in range(2)]
-            for dx in range(TAPS):
-                for dy in range(TAPS):
-                    first = max(0, REACH - dy)
-                    last = min(SIDE - 1, SIDE - 1 + REACH - dy)
-                    product = products[dy][dx % 2]
+            total = psum.tile([P, SIDE, 2, SIDE], F32, tag="aux")
+            nc.tensor.transpose(total[:].rearrange("p i gl j -> p (i gl j)"), turned_sum[:], ident[:])
+            rec = ends.tile([P, SIDE, 2, SIDE], F32)
+            nc.vector.reciprocal(out=rec[:], in_=total[:])
+            result = ends.tile([P, 2, SHARE, SIDE, SIDE], F32)
+            for half in range(2):
+                some = slice(4 * half, 4 * half + 4)
+                back = psum.tile([P, 4, 2, SHARE, SIDE], F32, tag="aux")
+                for r in range(4):
+                    nc.tensor.transpose(
+                        back[:, r].rearrange("p gl c j -> p (gl c j)"), turned[:, 4 * half + r, :], ident[:]
+                    )
+                for gl in range(2):
                     nc.vector.tensor_tensor(
-                        out=product[:, first : last + 1, :, :],
-                        in0=rows[hh][
-                            :, 2 * t + gl, :, first + dy - REACH : last + dy - REACH + 1, dx : dx + SIDE
-                        ].rearrange("p c i j -> p i c j"),
-                        in1=taps[:, dy, dx, first : last + 1, :]
-                        .unsqueeze(2)
-                        .to_broadcast([P, last + 1 - first, SHARE, SIDE]),
+                        out=result[:, gl, :, some, :],
+                        in0=back[:, :, gl].rearrange("p i c j -> p c i j"),
+                        in1=rec[:, some, gl, :].unsqueeze(1).to_broadcast([P, SHARE, 4, SIDE]),
                         op=ALU.mult,
                     )
-                    pieces = range(first // 2, last // 2 + 1)
-                    for q in pieces:
+            for gl in range(2):
+                nc.sync.dma_start(
+                    out=out_view[2 * t + gl, hh], in_=result[:, gl].rearrange("p c i j -> p (c i j)")
+                )
+
+        def window_sum(hh, t, e, waiting):
+            taps = e[:].rearrange("p (dy dx) i gl j -> p dy dx i gl j", dx=TAPS)
+            sums = [psum.tile([P, SIDE // 2, P], F32, tag="acc", bufs=4, name="sums%d" % bank) for bank in range(2)]
+            for dx in range(TAPS):
+                for dy in range(TAPS):
+                    lines = range(max(0, REACH - dy), min(SIDE - 1, SIDE - 1 + REACH - dy) + 1)
+                    first, count = lines[0], len(lines)
+                    product = stream.tile([P, SIDE, 2, SHARE, SIDE], F32, bufs=DEPTH)
+                    nc.vector.tensor_tensor(
+                        out=product[:, first : first + count],
+                        in0=rows[hh][
+                            :, 2 * t : 2 * t + 2, :, first + dy - REACH : first + dy - REACH + count, dx : dx + SIDE
+                        ].rearrange("p gl c i j -> p i gl c j"),
+                        in1=taps[:, dy, dx, first : first + count]
+                        .unsqueeze(3)
+                        .to_broadcast([P, count, 2, SHARE, SIDE]),
+                        op=ALU.mult,
+                    )
+                    for i in lines:
                         nc.tensor.matmul(
-                            out=sums[q % 2][:, q // 2, :],
-                            lhsT=product[:, 2 * q : 2 * q + 2].rearrange("p i c j -> p (i c j)"),
+                            out=sums[i % 2][:, i // 2, :],
+                            lhsT=product[:, i].rearrange("p gl c j -> p (gl c j)"),
                             rhs=ident[:],
                             is_transpose=True,
-                            start=(dx == 0 and dy == 0 and q in pieces[:2]),
-                            stop=(dx == TAPS - 1 and dy == TAPS - 1 and q in pieces[-2:]),
+                            start=(dx == 0 and dy == 0 and i in lines[:2]),
+                            stop=(dx == TAPS - 1 and dy == TAPS - 1 and i in lines[-2:]),
                         )
                 if dx == 0 and waiting:
                     finish(*waiting)
@@ -262,12 +247,10 @@ def tile_sam_pb_kernel(tc, logits, x, w3c, b3c, out):
         waiting = None
         for index, (hh, t) in enumerate(chunks):
             e = weights[index % 2]
-            sums = window_sum(hh, t, 0, e, waiting)
-            waiting = (hh, t, 0, sums, turned_sums[index % 2][0])
+            sums = window_sum(hh, t, e, waiting)
+            waiting = (hh, t, sums, turned_sums[index % 2])
             if index == 0:
                 project(1, range(0, 4))
-            sums = window_sum(hh, t, 1, e, waiting)
-            waiting = (hh, t, 1, sums, turned_sums[index % 2][1])
             if index + 2 < len(chunks):
                 shifted_exponentials(*chunks[index + 2], e)
                 fold_mirrored_rows(e)

@@ -83,7 +83,6 @@ def tile_sam_pb_kernel(tc, logits, x, w3c, b3c, out):
                     if mirrored(u) != u:
                         twin = taps[:, mirrored(u) - i + REACH, :, i, :]
                         nc.vector.tensor_tensor(out=twin, in0=twin, in1=taps[:, dy, :, i, :], op=ALU.add)
-                        nc.gpsimd.memset(taps[:, dy, :, i, :], 0.0)
 
         bias_bf = keep.tile([P, 2, SHARE], BF16)
         nc.sync.dma_start(out=bias_bf[:], in_=b3c.rearrange("(hh k c) -> k hh c", hh=2, k=P, c=SHARE))
@@ -154,9 +153,7 @@ def tile_sam_pb_kernel(tc, logits, x, w3c, b3c, out):
                     )
                 pair = rows[hh][:, :, 2 * cp : 2 * cp + 2]
                 for q in list(range(REACH)) + list(range(REACH + SIDE, WIDE)):
-                    nc.gpsimd.tensor_copy(
-                        out=pair[:, :, :, :, q], in_=pair[:, :, :, :, mirrored(q - REACH) + REACH]
-                    )
+                    nc.scalar.copy(out=pair[:, :, :, :, q], in_=pair[:, :, :, :, mirrored(q - REACH) + REACH])
 
         out_view = out.rearrange("b (hh k c) i j -> b hh k (c i j)", hh=2, k=P, c=SHARE)
 
@@ -241,9 +238,9 @@ def tile_sam_pb_kernel(tc, logits, x, w3c, b3c, out):
         project(0, range(0, 2))
         shifted_exponentials(*chunks[1], weights[1])
         project(0, range(2, 4))
+        turned_sums = [numerator_sums(weights[0]), numerator_sums(weights[1])]
         fold_mirrored_rows(weights[0])
         fold_mirrored_rows(weights[1])
-        turned_sums = [numerator_sums(weights[0]), numerator_sums(weights[1])]
         waiting = None
         for index, (hh, t) in enumerate(chunks):
             e = weights[index % 2]
@@ -253,6 +250,6 @@ def tile_sam_pb_kernel(tc, logits, x, w3c, b3c, out):
                 project(1, range(0, 4))
             if index + 2 < len(chunks):
                 shifted_exponentials(*chunks[index + 2], e)
-                fold_mirrored_rows(e)
                 turned_sums[index % 2] = numerator_sums(e)
+                fold_mirrored_rows(e)
         finish(*waiting)

@@ -36,7 +36,6 @@ def tile_sam_pb_kernel(tc, logits, x, w3c, b3c, out):
         keep = stack.enter_context(tc.tile_pool(name="keep", bufs=1))
         loads = stack.enter_context(tc.tile_pool(name="loads", bufs=2))
         stream = stack.enter_context(tc.tile_pool(name="stream", bufs=2))
-        ends = stack.enter_context(tc.tile_pool(name="ends", bufs=2))
         psum = stack.enter_context(tc.psum_pool(name="psum", bufs=2))
 
         ident = keep.tile([P, P], F32)
@@ -89,24 +88,29 @@ def tile_sam_pb_kernel(tc, logits, x, w3c, b3c, out):
         bias = keep.tile([P, 2, SHARE], F32)
         nc.scalar.copy(out=bias[:], in_=bias_bf[:])
 
-        raw_x = keep.tile([P, 32, 128], BF16)
-        nc.sync.dma_start(
-            out=raw_x[:],
-            in_=x.rearrange("b (g u p e) i j -> p (b g u) (e i j)", g=4, u=2, p=P, e=2),
-        )
-        grouped_x = keep.tile([P, 4, 4, SPOTS, 4], BF16, align_bytes=64)
-        raw_view = raw_x[:].rearrange("p (b g u) (e n) -> p g b n (u e)", b=4, g=4, u=2, e=2)
-        for g in range(4):
-            nc.scalar.copy(out=grouped_x[:, g], in_=raw_view[:, g])
         codes_x = keep.tile([P, 4, 256], U32, align_bytes=64)
         scales_x = keep.tile([P, 4, 256], U8, align_bytes=64)
-        nc.vector.quantize_mx(
-            out=codes_x[:].rearrange("p g n -> p (g n)").bitcast(FP8X4),
-            scales=scales_x[:].rearrange("p g n -> p (g n)"),
-            in_=grouped_x[:].rearrange("p g b n f -> p (g b n f)"),
-        )
+        with tc.tile_pool(name="once", bufs=1) as once:
+            raw_x = once.tile([P, 32, 128], BF16)
+            nc.sync.dma_start(
+                out=raw_x[:],
+                in_=x.rearrange("b (g u p e) i j -> p (b g u) (e i j)", g=4, u=2, p=P, e=2),
+            )
+            grouped_x = once.tile([P, 4, 4, SPOTS, 4], BF16, align_bytes=64)
+            raw_view = raw_x[:].rearrange("p (b g u) (e n) -> p g b n (u e)", b=4, g=4, u=2, e=2)
+            for g in range(4):
+                nc.scalar.copy(out=grouped_x[:, g], in_=raw_view[:, g])
+            nc.vector.quantize_mx(
+                out=codes_x[:].rearrange("p g n -> p (g n)").bitcast(FP8X4),
+                scales=scales_x[:].rearrange("p g n -> p (g n)"),
+                in_=grouped_x[:].rearrange("p g b n f -> p (g b n f)"),
+            )
+        flow = stack.enter_context(tc.tile_pool(name="flow", bufs=DEPTH))
+        ends = stack.enter_context(tc.tile_pool(name="ends", bufs=2))
 
         rows = [keep.tile([P, 4, SHARE, SIDE, WIDE], F32, name="rows%d" % hh) for hh in range(2)]
+        ROWS_WORDS = 4 * SHARE * SIDE * WIDE
+        nudged = [keep.tile([P, ROWS_WORDS + 2], F32, name="nudged%d" % hh) for hh in range(2)]
         w_view = w3c.rearrange("(hh k c) q -> hh k c q", hh=2, k=P, c=SHARE)
 
         def project(hh, pairs):
@@ -154,6 +158,13 @@ def tile_sam_pb_kernel(tc, logits, x, w3c, b3c, out):
                 pair = rows[hh][:, :, 2 * cp : 2 * cp + 2]
                 for q in list(range(REACH)) + list(range(REACH + SIDE, WIDE)):
                     nc.scalar.copy(out=pair[:, :, :, :, q], in_=pair[:, :, :, :, mirrored(q - REACH) + REACH])
+
+        def nudge(hh):
+            for t in range(2):
+                nc.scalar.copy(
+                    out=nudged[hh][:, 1 + t * ROWS_WORDS // 2 : 1 + (t + 1) * ROWS_WORDS // 2],
+                    in_=rows[hh][:, 2 * t : 2 * t + 2].rearrange("p b c i q -> p (b c i q)"),
+                )
 
         out_view = out.rearrange("b (hh k c) i j -> b hh k (c i j)", hh=2, k=P, c=SHARE)
 
@@ -204,15 +215,19 @@ def tile_sam_pb_kernel(tc, logits, x, w3c, b3c, out):
 
         def window_sum(hh, t, e, waiting):
             taps = e[:].rearrange("p (dy dx) i gl j -> p dy dx i gl j", dx=TAPS)
+            aligned = [
+                rows[hh][:],
+                nudged[hh][:, 1 : 1 + ROWS_WORDS].rearrange("p (b c i q) -> p b c i q", b=4, c=SHARE, i=SIDE),
+            ]
             sums = [psum.tile([P, SIDE // 2, P], F32, tag="acc", bufs=4, name="sums%d" % bank) for bank in range(2)]
             for dx in range(TAPS):
                 for dy in range(TAPS):
                     lines = range(max(0, REACH - dy), min(SIDE - 1, SIDE - 1 + REACH - dy) + 1)
                     first, count = lines[0], len(lines)
-                    product = stream.tile([P, SIDE, 2, SHARE, SIDE], F32, bufs=DEPTH)
+                    product = flow.tile([P, SIDE, 2, SHARE, SIDE], F32)
                     nc.vector.tensor_tensor(
                         out=product[:, first : first + count],
-                        in0=rows[hh][
+                        in0=aligned[dx % 2][
                             :, 2 * t : 2 * t + 2, :, first + dy - REACH : first + dy - REACH + count, dx : dx + SIDE
                         ].rearrange("p gl c i j -> p i gl c j"),
                         in1=taps[:, dy, dx, first : first + count]
@@ -238,6 +253,7 @@ def tile_sam_pb_kernel(tc, logits, x, w3c, b3c, out):
         project(0, range(0, 2))
         shifted_exponentials(*chunks[1], weights[1])
         project(0, range(2, 4))
+        nudge(0)
         turned_sums = [numerator_sums(weights[0]), numerator_sums(weights[1])]
         fold_mirrored_rows(weights[0])
         fold_mirrored_rows(weights[1])
@@ -248,6 +264,7 @@ def tile_sam_pb_kernel(tc, logits, x, w3c, b3c, out):
             waiting = (hh, t, sums, turned_sums[index % 2])
             if index == 0:
                 project(1, range(0, 4))
+                nudge(1)
             if index + 2 < len(chunks):
                 shifted_exponentials(*chunks[index + 2], e)
                 turned_sums[index % 2] = numerator_sums(e)

@@ -16,9 +16,10 @@ SIDE = 8
 SPOTS = SIDE * SIDE
 TAPS = 7
 REACH = TAPS // 2
-WIDE = SIDE + 2 * REACH
 SHARE = 8
-DEPTH = 7
+HALF = SHARE // 2
+SPARE = 2
+GPSIMD_DX = (3,)
 FLOPS = 2 * 2048 * 2048 * 256 + 2 * 4 * 2048 * 64 * 49
 
 
@@ -28,6 +29,11 @@ def mirrored(u):
     if u > SIDE - 1:
         return 2 * (SIDE - 1) - u
     return u
+
+
+def inside(d):
+    first = max(0, REACH - d)
+    return first, min(SIDE, SIDE + REACH - d) - first
 
 
 def tile_sam_pb_kernel(tc, logits, x, w3c, b3c, out):
@@ -41,12 +47,15 @@ def tile_sam_pb_kernel(tc, logits, x, w3c, b3c, out):
         ident = keep.tile([P, P], F32)
         make_identity(nc, ident[:])
 
-        weights = [keep.tile([P, TAPS * TAPS, SIDE, 2, SIDE], F32, name="weights%d" % r) for r in range(2)]
+        weights = [keep.tile([P, TAPS * TAPS, SPOTS, 2], F32, name="weights%d" % r) for r in range(2)]
 
-        def shifted_exponentials(hh, t, e):
+        def load_logits(hh, t):
             lt = loads.tile([P, 2, TAPS * TAPS, SPOTS], BF16)
             for gl in range(2):
                 nc.sync.dma_start(out=lt[:, gl], in_=logits[2 * t + gl, hh * P : (hh + 1) * P])
+            return lt
+
+        def shifted_exponentials(lt, e):
             top = keep.tile([P, 2, 24, SPOTS], BF16)
             nc.vector.tensor_tensor(out=top[:], in0=lt[:, :, 0:24, :], in1=lt[:, :, 24:48, :], op=ALU.max)
             width = 24
@@ -62,31 +71,40 @@ def tile_sam_pb_kernel(tc, logits, x, w3c, b3c, out):
             nc.vector.tensor_tensor(
                 out=top[:, :, 0:1, :], in0=top[:, :, 0:1, :], in1=lt[:, :, 48:49, :], op=ALU.max
             )
-            for gl in range(2):
+            for part in (slice(0, 24), slice(24, 49)):
+                count = part.stop - part.start
                 nc.vector.tensor_tensor(
-                    out=e[:, :, :, gl, :],
-                    in0=lt[:, gl].rearrange("p l (i j) -> p l i j", j=SIDE),
-                    in1=top[:, gl, 0:1, :]
-                    .rearrange("p l (i j) -> p l i j", j=SIDE)
-                    .to_broadcast([P, TAPS * TAPS, SIDE, SIDE]),
+                    out=e[:, part],
+                    in0=lt[:, :, part].rearrange("p gl l n -> p l n gl"),
+                    in1=top[:, :, 0]
+                    .rearrange("p gl n -> p n gl")
+                    .unsqueeze(1)
+                    .to_broadcast([P, count, SPOTS, 2]),
                     op=ALU.subtract,
                 )
-            flat = e[:].rearrange("p l i gl j -> p (l i gl j)")
-            nc.scalar.activation(out=flat, in_=flat, func=ACT.Exp)
+                flat = e[:, part].rearrange("p l n gl -> p (l n gl)")
+                nc.scalar.activation(out=flat, in_=flat, func=ACT.Exp)
 
-        def fold_mirrored_rows(e):
-            taps = e[:].rearrange("p (dy dx) i gl j -> p dy dx i (gl j)", dx=TAPS)
-            for i in range(SIDE):
-                for dy in range(TAPS):
-                    u = i + dy - REACH
+        def fold_mirrored(e):
+            taps = e[:].rearrange("p (dy dx) (i j) gl -> p dy dx i j gl", dx=TAPS, j=SIDE)
+            pairs = []
+            for s in range(SIDE):
+                for d in range(TAPS):
+                    u = s + d - REACH
                     if mirrored(u) != u:
-                        twin = taps[:, mirrored(u) - i + REACH, :, i, :]
-                        nc.vector.tensor_tensor(out=twin, in0=twin, in1=taps[:, dy, :, i, :], op=ALU.add)
+                        pairs.append((s, d, mirrored(u) - s + REACH))
+            for i, dy, twin_dy in pairs:
+                twin = taps[:, twin_dy, :, i].rearrange("p dx j gl -> p dx (j gl)")
+                nc.vector.tensor_tensor(
+                    out=twin, in0=twin, in1=taps[:, dy, :, i].rearrange("p dx j gl -> p dx (j gl)"), op=ALU.add
+                )
+            for j, dx, twin_dx in pairs:
+                twin = taps[:, :, twin_dx, :, j]
+                nc.vector.tensor_tensor(out=twin, in0=twin, in1=taps[:, :, dx, :, j], op=ALU.add)
 
+        first_logits = load_logits(0, 0)
         bias_bf = keep.tile([P, 2, SHARE], BF16)
-        nc.sync.dma_start(out=bias_bf[:], in_=b3c.rearrange("(hh k c) -> k hh c", hh=2, k=P, c=SHARE))
         bias = keep.tile([P, 2, SHARE], F32)
-        nc.scalar.copy(out=bias[:], in_=bias_bf[:])
 
         codes_x = keep.tile([P, 4, 256], U32, align_bytes=64)
         scales_x = keep.tile([P, 4, 256], U8, align_bytes=64)
@@ -96,84 +114,92 @@ def tile_sam_pb_kernel(tc, logits, x, w3c, b3c, out):
                 out=raw_x[:],
                 in_=x.rearrange("b (g u p e) i j -> p (b g u) (e i j)", g=4, u=2, p=P, e=2),
             )
-            grouped_x = once.tile([P, 4, 4, SPOTS, 4], BF16, align_bytes=64)
-            raw_view = raw_x[:].rearrange("p (b g u) (e n) -> p g b n (u e)", b=4, g=4, u=2, e=2)
+            nc.sync.dma_start(out=bias_bf[:], in_=b3c.rearrange("(hh k c) -> k hh c", hh=2, k=P, c=SHARE))
+            grouped_x = once.tile([P, 4, 2, SPOTS, 2, 4], BF16, align_bytes=64)
+            raw_view = raw_x[:].rearrange("p (t gl g u) (e n) -> p g t n gl (u e)", t=2, gl=2, g=4, u=2, e=2)
             for g in range(4):
-                nc.scalar.copy(out=grouped_x[:, g], in_=raw_view[:, g])
+                for t in range(2):
+                    nc.scalar.copy(out=grouped_x[:, g, t], in_=raw_view[:, g, t])
             nc.vector.quantize_mx(
                 out=codes_x[:].rearrange("p g n -> p (g n)").bitcast(FP8X4),
                 scales=scales_x[:].rearrange("p g n -> p (g n)"),
-                in_=grouped_x[:].rearrange("p g b n f -> p (g b n f)"),
+                in_=grouped_x[:].rearrange("p g t n gl f -> p (g t n gl f)"),
             )
-        flow = stack.enter_context(tc.tile_pool(name="flow", bufs=DEPTH))
+        nc.scalar.copy(out=bias[:], in_=bias_bf[:])
+        flow = stack.enter_context(tc.tile_pool(name="flow", bufs=1))
         ends = stack.enter_context(tc.tile_pool(name="ends", bufs=2))
 
-        rows = [keep.tile([P, 4, SHARE, SIDE, WIDE], F32, name="rows%d" % hh) for hh in range(2)]
-        ROWS_WORDS = 4 * SHARE * SIDE * WIDE
-        nudged = [keep.tile([P, ROWS_WORDS + 2], F32, name="nudged%d" % hh) for hh in range(2)]
+        products = []
+        for dx in range(TAPS):
+            first, count = inside(dx)
+            spares = [flow.tile([P, SIDE, SIDE, 2 * SHARE], F32, name="product%d_%d" % (dx, s)) for s in range(SPARE)]
+            for spare in spares:
+                if first > 0:
+                    nc.gpsimd.memset(spare[:, :, 0:first, :], 0.0)
+                if first + count < SIDE:
+                    nc.gpsimd.memset(spare[:, :, first + count : SIDE, :], 0.0)
+            products.append(spares)
+
         w_view = w3c.rearrange("(hh k c) q -> hh k c q", hh=2, k=P, c=SHARE)
 
-        def project(hh, pairs):
-            for cp in pairs:
-                w_sb = stream.tile([P, 2, 2048], BF16)
-                nc.sync.dma_start(out=w_sb[:], in_=w_view[hh][:, 2 * cp : 2 * cp + 2, :])
-                grouped_w = stream.tile([P, 4, 256, 4], BF16, align_bytes=64)
-                for g in range(4):
-                    wt = psum.tile([P, 2, 256], F32, tag="proj")
-                    for u in range(2):
-                        for cl in range(2):
-                            words = w_sb[:, cl, :].bitcast(F32)
-                            nc.tensor.transpose(
-                                wt[:, u, cl * P : (cl + 1) * P],
-                                words[:, (2 * g + u) * P : (2 * g + u + 1) * P],
-                                ident[:],
-                            )
-                    nc.scalar.copy(out=grouped_w[:, g].bitcast(F32), in_=wt[:].rearrange("p u o -> p o u"))
-                codes_w = stream.tile([P, 4, 256], U32, align_bytes=64)
-                scales_w = stream.tile([P, 4, 256], U8, align_bytes=64)
-                nc.vector.quantize_mx(
-                    out=codes_w[:].rearrange("p g o -> p (g o)").bitcast(FP8X4),
-                    scales=scales_w[:].rearrange("p g o -> p (g o)"),
-                    in_=grouped_w[:].rearrange("p g o f -> p (g o f)"),
-                )
-                for cl in range(2):
-                    c = 2 * cp + cl
-                    x3 = psum.tile([P, 4, SIDE, SIDE], F32, tag="proj")
+        def quantised_weights(hh, cp):
+            w_sb = stream.tile([P, 2, 2048], BF16)
+            nc.sync.dma_start(out=w_sb[:], in_=w_view[hh][:, 2 * cp : 2 * cp + 2, :])
+            grouped_w = stream.tile([P, 4, 256, 4], BF16, align_bytes=64)
+            for g in range(4):
+                wt = psum.tile([P, 2, 256], F32, tag="aux")
+                for u in range(2):
+                    for cl in range(2):
+                        words = w_sb[:, cl, :].bitcast(F32)
+                        nc.tensor.transpose(
+                            wt[:, u, cl * P : (cl + 1) * P],
+                            words[:, (2 * g + u) * P : (2 * g + u + 1) * P],
+                            ident[:],
+                        )
+                nc.scalar.copy(out=grouped_w[:, g].bitcast(F32), in_=wt[:].rearrange("p u o -> p o u"))
+            codes_w = stream.tile([P, 4, 256], U32, align_bytes=64, bufs=4)
+            scales_w = stream.tile([P, 4, 256], U8, align_bytes=64, bufs=4)
+            nc.vector.quantize_mx(
+                out=codes_w[:].rearrange("p g o -> p (g o)").bitcast(FP8X4),
+                scales=scales_w[:].rearrange("p g o -> p (g o)"),
+                in_=grouped_w[:].rearrange("p g o f -> p (g o f)"),
+            )
+            return codes_w, scales_w
+
+        def project(t, quantised):
+            spread = ends.tile([P, SPOTS * 2, SHARE], F32)
+            banks = []
+            columns = slice(t * P, (t + 1) * P)
+            for half in range(2):
+                bank = psum.tile([P, HALF, P], F32, tag="x3", bufs=4)
+                for r in range(HALF):
+                    c = half * HALF + r
+                    codes_w, scales_w = quantised[c // 2]
+                    own = slice((c % 2) * P, (c % 2 + 1) * P)
                     for g in range(4):
                         nc.tensor.matmul_mx(
-                            out=x3[:].rearrange("p b i j -> p (b i j)"),
-                            lhsT=codes_w[:, g, cl * P : (cl + 1) * P].bitcast(FP8X4),
-                            lhsT_scale=scales_w[:, g, cl * P : (cl + 1) * P],
-                            rhs=codes_x[:, g, :].bitcast(FP8X4),
-                            rhs_scale=scales_x[:, g, :],
+                            out=bank[:, r, :],
+                            lhsT=codes_w[:, g, own].bitcast(FP8X4),
+                            lhsT_scale=scales_w[:, g, own],
+                            rhs=codes_x[:, g, columns].bitcast(FP8X4),
+                            rhs_scale=scales_x[:, g, columns],
                             start=(g == 0),
                             stop=(g == 3),
                         )
-                    nc.scalar.activation(
-                        out=rows[hh][:, :, c, :, REACH : REACH + SIDE],
-                        in_=x3[:],
-                        func=ACT.Identity,
-                        bias=bias[:, hh, c : c + 1],
-                    )
-                pair = rows[hh][:, :, 2 * cp : 2 * cp + 2]
-                for q in list(range(REACH)) + list(range(REACH + SIDE, WIDE)):
-                    nc.scalar.copy(out=pair[:, :, :, :, q], in_=pair[:, :, :, :, mirrored(q - REACH) + REACH])
-
-        def nudge(hh):
-            for t in range(2):
                 nc.scalar.copy(
-                    out=nudged[hh][:, 1 + t * ROWS_WORDS // 2 : 1 + (t + 1) * ROWS_WORDS // 2],
-                    in_=rows[hh][:, 2 * t : 2 * t + 2].rearrange("p b c i q -> p (b c i q)"),
+                    out=spread[:, :, half * HALF : (half + 1) * HALF], in_=bank[:].rearrange("p c s -> p s c")
                 )
+                banks.append(bank)
+            return banks, spread
 
-        out_view = out.rearrange("b (hh k c) i j -> b hh k (c i j)", hh=2, k=P, c=SHARE)
+        out_view = out.rearrange("b (hh k c) i j -> hh k b c (i j)", hh=2, k=P, c=SHARE)
 
         def numerator_sums(e):
             both = psum.tile([P, P], F32, tag="aux")
             for tap in range(TAPS * TAPS):
                 nc.tensor.matmul(
                     out=both[:],
-                    lhsT=e[:, tap].rearrange("p i gl j -> p (i gl j)"),
+                    lhsT=e[:, tap].rearrange("p n gl -> p (n gl)"),
                     rhs=ident[:],
                     is_transpose=True,
                     start=(tap == 0),
@@ -189,84 +215,151 @@ def tile_sam_pb_kernel(tc, logits, x, w3c, b3c, out):
                 nc.scalar.copy(
                     out=turned[:].rearrange("p (h bank) k -> p bank h k", bank=2)[:, bank], in_=sums[bank][:]
                 )
-            total = psum.tile([P, SIDE, 2, SIDE], F32, tag="aux")
-            nc.tensor.transpose(total[:].rearrange("p i gl j -> p (i gl j)"), turned_sum[:], ident[:])
-            rec = ends.tile([P, SIDE, 2, SIDE], F32)
-            nc.vector.reciprocal(out=rec[:], in_=total[:])
+            total = psum.tile([P, P], F32, tag="aux")
+            nc.tensor.transpose(total[:], turned_sum[:], ident[:])
+            rec = ends.tile([P, SIDE, SIDE, 2], F32)
+            nc.vector.reciprocal(out=rec[:].rearrange("p i j gl -> p (i j gl)"), in_=total[:])
             result = ends.tile([P, 2, SHARE, SIDE, SIDE], F32)
             for half in range(2):
                 some = slice(4 * half, 4 * half + 4)
-                back = psum.tile([P, 4, 2, SHARE, SIDE], F32, tag="aux")
+                back = psum.tile([P, 4, SIDE, 2, SHARE], F32, tag="aux")
                 for r in range(4):
                     nc.tensor.transpose(
-                        back[:, r].rearrange("p gl c j -> p (gl c j)"), turned[:, 4 * half + r, :], ident[:]
+                        back[:, r].rearrange("p j gl c -> p (j gl c)"), turned[:, 4 * half + r, :], ident[:]
                     )
                 for gl in range(2):
                     nc.vector.tensor_tensor(
                         out=result[:, gl, :, some, :],
-                        in0=back[:, :, gl].rearrange("p i c j -> p c i j"),
-                        in1=rec[:, some, gl, :].unsqueeze(1).to_broadcast([P, SHARE, 4, SIDE]),
+                        in0=back[:, :, :, gl].rearrange("p i j c -> p c i j"),
+                        in1=rec[:, some, :, gl].unsqueeze(1).to_broadcast([P, SHARE, 4, SIDE]),
                         op=ALU.mult,
                     )
+            for c in range(SHARE):
+                lane = result[:, :, c].rearrange("p gl i j -> p gl (i j)")
+                nc.scalar.activation(out=lane, in_=lane, func=ACT.Identity, bias=bias[:, hh, c : c + 1])
             for gl in range(2):
                 nc.sync.dma_start(
-                    out=out_view[2 * t + gl, hh], in_=result[:, gl].rearrange("p c i j -> p (c i j)")
+                    out=out_view[hh, :, 2 * t + gl], in_=result[:, gl].rearrange("p c i j -> p c (i j)")
                 )
 
-        def window_sum(hh, t, e, waiting):
-            taps = e[:].rearrange("p (dy dx) i gl j -> p dy dx i gl j", dx=TAPS)
-            aligned = [
-                rows[hh][:],
-                nudged[hh][:, 1 : 1 + ROWS_WORDS].rearrange("p (b c i q) -> p b c i q", b=4, c=SHARE, i=SIDE),
-            ]
-            sums = [psum.tile([P, SIDE // 2, P], F32, tag="acc", bufs=4, name="sums%d" % bank) for bank in range(2)]
-            for dx in range(TAPS):
-                for dy in range(TAPS):
-                    lines = range(max(0, REACH - dy), min(SIDE - 1, SIDE - 1 + REACH - dy) + 1)
-                    first, count = lines[0], len(lines)
-                    product = flow.tile([P, SIDE, 2, SHARE, SIDE], F32)
-                    nc.vector.tensor_tensor(
-                        out=product[:, first : first + count],
-                        in0=aligned[dx % 2][
-                            :, 2 * t : 2 * t + 2, :, first + dy - REACH : first + dy - REACH + count, dx : dx + SIDE
-                        ].rearrange("p gl c i j -> p i gl c j"),
-                        in1=taps[:, dy, dx, first : first + count]
+        def window_sum(e, banks, spread, between):
+            taps = e[:].rearrange("p (dy dx) (i j) gl -> p dy dx i (j gl)", dx=TAPS, j=SIDE)
+            sources = [bank[:].rearrange("p c (i s) -> p i s c", i=SIDE) for bank in banks]
+            spread_rows = spread[:].rearrange("p (i s) c -> p i s c", i=SIDE)
+            sums = [psum.tile([P, SIDE // 2, P], F32, tag="acc", name="sums%d" % bank) for bank in range(2)]
+            opened = set()
+            left = [sum(1 for dy in range(TAPS) for i in range(SIDE) if 0 <= i + dy - REACH < SIDE and i % 2 == b) * TAPS for b in range(2)]
+
+            def add(dy, product):
+                first, count = inside(dy)
+                for i in range(first, first + count):
+                    bank = i % 2
+                    left[bank] -= 1
+                    nc.tensor.matmul(
+                        out=sums[bank][:, i // 2, :],
+                        lhsT=product[:, i].rearrange("p j s -> p (j s)"),
+                        rhs=ident[:],
+                        is_transpose=True,
+                        start=(bank not in opened),
+                        stop=(left[bank] == 0),
+                    )
+                    opened.add(bank)
+
+            late = []
+            for dy in range(TAPS):
+                i0, rows = inside(dy)
+                lines = slice(i0, i0 + rows)
+                source_lines = slice(i0 + dy - REACH, i0 + dy - REACH + rows)
+                new_late = []
+                for dx in GPSIMD_DX:
+                    j0, columns = inside(dx)
+                    product = products[dx][dy % SPARE]
+                    s0, s1 = 2 * (j0 + dx - REACH), 2 * (j0 + dx - REACH + columns)
+                    nc.gpsimd.tensor_tensor(
+                        out=product[:, lines, j0 : j0 + columns].rearrange("p i j (gl c) -> p i (j gl) c", gl=2),
+                        in0=spread_rows[:, source_lines, s0:s1],
+                        in1=taps[:, dy, dx, lines, 2 * j0 : 2 * (j0 + columns)]
                         .unsqueeze(3)
-                        .to_broadcast([P, count, 2, SHARE, SIDE]),
+                        .to_broadcast([P, rows, 2 * columns, SHARE]),
                         op=ALU.mult,
                     )
-                    for i in lines:
-                        nc.tensor.matmul(
-                            out=sums[i % 2][:, i // 2, :],
-                            lhsT=product[:, i].rearrange("p gl c j -> p (gl c j)"),
-                            rhs=ident[:],
-                            is_transpose=True,
-                            start=(dx == 0 and dy == 0 and i in lines[:2]),
-                            stop=(dx == TAPS - 1 and dy == TAPS - 1 and i in lines[-2:]),
+                    new_late.append((dy, product))
+                for dx in range(TAPS):
+                    if dx in GPSIMD_DX:
+                        continue
+                    j0, columns = inside(dx)
+                    product = products[dx][dy % SPARE]
+                    s0, s1 = 2 * (j0 + dx - REACH), 2 * (j0 + dx - REACH + columns)
+                    for half in range(2):
+                        nc.vector.tensor_tensor(
+                            out=product[:, lines, j0 : j0 + columns].rearrange("p i j (gl c) -> p i (j gl) c", gl=2)[
+                                :, :, :, half * HALF : (half + 1) * HALF
+                            ],
+                            in0=sources[half][:, source_lines, s0:s1],
+                            in1=taps[:, dy, dx, lines, 2 * j0 : 2 * (j0 + columns)]
+                            .unsqueeze(3)
+                            .to_broadcast([P, rows, 2 * columns, HALF]),
+                            op=ALU.mult,
                         )
-                if dx == 0 and waiting:
-                    finish(*waiting)
+                    add(dy, product)
+                for old in late:
+                    add(*old)
+                late = new_late
+                if dy in between:
+                    between[dy]()
+            for old in late:
+                add(*old)
             return sums
 
         chunks = [(hh, t) for hh in range(2) for t in range(2)]
-        shifted_exponentials(*chunks[0], weights[0])
-        project(0, range(0, 2))
-        shifted_exponentials(*chunks[1], weights[1])
-        project(0, range(2, 4))
-        nudge(0)
-        turned_sums = [numerator_sums(weights[0]), numerator_sums(weights[1])]
-        fold_mirrored_rows(weights[0])
-        fold_mirrored_rows(weights[1])
-        waiting = None
-        for index, (hh, t) in enumerate(chunks):
+        state = {"waiting": None}
+        quantised = [quantised_weights(0, 0)]
+        shifted_exponentials(first_logits, weights[0])
+        for cp in range(1, 4):
+            quantised.append(quantised_weights(0, cp))
+        second_logits = load_logits(0, 1)
+        turned_sums = {0: numerator_sums(weights[0])}
+        fold_mirrored(weights[0])
+        ready = {0: project(0, quantised)}
+
+        def softmax(index, lt):
             e = weights[index % 2]
-            sums = window_sum(hh, t, e, waiting)
-            waiting = (hh, t, sums, turned_sums[index % 2])
-            if index == 0:
-                project(1, range(0, 4))
-                nudge(1)
-            if index + 2 < len(chunks):
-                shifted_exponentials(*chunks[index + 2], e)
-                turned_sums[index % 2] = numerator_sums(e)
-                fold_mirrored_rows(e)
-        finish(*waiting)
+            shifted_exponentials(lt, e)
+            turned_sums[index] = numerator_sums(e)
+            fold_mirrored(e)
+
+        def end_waiting():
+            if state["waiting"]:
+                finish(*state["waiting"])
+
+        def step_a():
+            ready[1] = project(1, quantised)
+            softmax(1, second_logits)
+            state["lt"] = load_logits(1, 0)
+
+        def step_b():
+            quantised[0:2] = [quantised_weights(1, cp) for cp in range(2)]
+
+        def step_c():
+            quantised[2:4] = [quantised_weights(1, cp) for cp in range(2, 4)]
+
+        def step_d():
+            softmax(2, state["lt"])
+            state["lt"] = load_logits(1, 1)
+            ready[2] = project(0, quantised)
+
+        def step_e():
+            ready[3] = project(1, quantised)
+            softmax(3, state["lt"])
+
+        plans = [
+            {0: step_a, 2: step_b, 4: step_c},
+            {0: end_waiting, 1: step_d},
+            {0: end_waiting, 1: step_e},
+            {0: end_waiting},
+        ]
+        for index, (hh, t) in enumerate(chunks):
+            banks, spread = ready[index]
+            sums = window_sum(weights[index % 2], banks, spread, plans[index])
+            state["waiting"] = (hh, t, sums, turned_sums[index])
+        end_waiting()

@@ -55,8 +55,8 @@ def tile_sam_pb_kernel(tc, logits, x, w3c, b3c, out):
                 nc.sync.dma_start(out=lt[:, gl], in_=logits[2 * t + gl, hh * P : (hh + 1) * P])
             return lt
 
-        def shifted_exponentials(lt, e):
-            top = keep.tile([P, 2, 24, SPOTS], BF16)
+        def largest(lt):
+            top = loads.tile([P, 2, 24, SPOTS], BF16)
             nc.vector.tensor_tensor(out=top[:], in0=lt[:, :, 0:24, :], in1=lt[:, :, 24:48, :], op=ALU.max)
             width = 24
             while width > 1:
@@ -71,36 +71,37 @@ def tile_sam_pb_kernel(tc, logits, x, w3c, b3c, out):
             nc.vector.tensor_tensor(
                 out=top[:, :, 0:1, :], in0=top[:, :, 0:1, :], in1=lt[:, :, 48:49, :], op=ALU.max
             )
-            for part in (slice(0, 24), slice(24, 49)):
-                count = part.stop - part.start
-                nc.vector.tensor_tensor(
-                    out=e[:, part],
-                    in0=lt[:, :, part].rearrange("p gl l n -> p l n gl"),
-                    in1=top[:, :, 0]
-                    .rearrange("p gl n -> p n gl")
-                    .unsqueeze(1)
-                    .to_broadcast([P, count, SPOTS, 2]),
-                    op=ALU.subtract,
-                )
-                flat = e[:, part].rearrange("p l n gl -> p (l n gl)")
-                nc.scalar.activation(out=flat, in_=flat, func=ACT.Exp)
+            return top
 
-        def fold_mirrored(e):
+        def shifted_exponentials(engine, lt, top, e, part):
+            count = part.stop - part.start
+            engine.tensor_tensor(
+                out=e[:, part],
+                in0=lt[:, :, part].rearrange("p gl l n -> p l n gl"),
+                in1=top[:, :, 0].rearrange("p gl n -> p n gl").unsqueeze(1).to_broadcast([P, count, SPOTS, 2]),
+                op=ALU.subtract,
+            )
+            flat = e[:, part].rearrange("p l n gl -> p (l n gl)")
+            nc.scalar.activation(out=flat, in_=flat, func=ACT.Exp)
+
+        folds = []
+        for s in range(SIDE):
+            for d in range(TAPS):
+                u = s + d - REACH
+                if mirrored(u) != u:
+                    folds.append((s, d, mirrored(u) - s + REACH))
+
+        def fold_rows(engine, e):
+            taps = e[:].rearrange("p (dy dx) (i j) gl -> p dy dx i (j gl)", dx=TAPS, j=SIDE)
+            for i, dy, twin_dy in folds:
+                twin = taps[:, twin_dy, :, i]
+                engine.tensor_tensor(out=twin, in0=twin, in1=taps[:, dy, :, i], op=ALU.add)
+
+        def fold_columns(engine, e):
             taps = e[:].rearrange("p (dy dx) (i j) gl -> p dy dx i j gl", dx=TAPS, j=SIDE)
-            pairs = []
-            for s in range(SIDE):
-                for d in range(TAPS):
-                    u = s + d - REACH
-                    if mirrored(u) != u:
-                        pairs.append((s, d, mirrored(u) - s + REACH))
-            for i, dy, twin_dy in pairs:
-                twin = taps[:, twin_dy, :, i].rearrange("p dx j gl -> p dx (j gl)")
-                nc.vector.tensor_tensor(
-                    out=twin, in0=twin, in1=taps[:, dy, :, i].rearrange("p dx j gl -> p dx (j gl)"), op=ALU.add
-                )
-            for j, dx, twin_dx in pairs:
+            for j, dx, twin_dx in folds:
                 twin = taps[:, :, twin_dx, :, j]
-                nc.vector.tensor_tensor(out=twin, in0=twin, in1=taps[:, :, dx, :, j], op=ALU.add)
+                engine.tensor_tensor(out=twin, in0=twin, in1=taps[:, :, dx, :, j], op=ALU.add)
 
         first_logits = load_logits(0, 0)
         bias_bf = keep.tile([P, 2, SHARE], BF16)
@@ -305,61 +306,54 @@ def tile_sam_pb_kernel(tc, logits, x, w3c, b3c, out):
                 for old in late:
                     add(*old)
                 late = new_late
-                if dy in between:
-                    between[dy]()
+                between(dy)
             for old in late:
                 add(*old)
             return sums
 
         chunks = [(hh, t) for hh in range(2) for t in range(2)]
-        state = {"waiting": None}
-        quantised = [quantised_weights(0, 0)]
-        shifted_exponentials(first_logits, weights[0])
-        for cp in range(1, 4):
-            quantised.append(quantised_weights(0, cp))
-        second_logits = load_logits(0, 1)
-        turned_sums = {0: numerator_sums(weights[0])}
-        fold_mirrored(weights[0])
-        ready = {0: project(0, quantised)}
+        parts = [slice(TAPS * dy, TAPS * dy + TAPS) for dy in range(TAPS)]
+        turned_sums, ready, quantised, logit_tiles, tops = {}, {}, {}, {0: first_logits}, {}
+        waiting = []
 
-        def softmax(index, lt):
+        quantised[0] = [quantised_weights(0, 0)]
+        tops[0] = largest(first_logits)
+        for part in (slice(0, 25), slice(25, 49)):
+            shifted_exponentials(nc.vector, first_logits, tops[0], weights[0], part)
+        quantised[0].extend(quantised_weights(0, cp) for cp in range(1, 4))
+        logit_tiles[1] = load_logits(0, 1)
+        turned_sums[0] = numerator_sums(weights[0])
+        fold_rows(nc.vector, weights[0])
+        fold_columns(nc.vector, weights[0])
+        ready[0] = project(0, quantised[0])
+
+        def prepare(index, dy):
             e = weights[index % 2]
-            shifted_exponentials(lt, e)
-            turned_sums[index] = numerator_sums(e)
-            fold_mirrored(e)
+            if dy == 0:
+                tops[index] = largest(logit_tiles[index])
+            if dy < 4:
+                for part in parts[2 * dy : 2 * dy + 2]:
+                    shifted_exponentials(nc.gpsimd, logit_tiles[index], tops[index], e, part)
+            if dy == 4:
+                turned_sums[index] = numerator_sums(e)
+                if index + 1 < len(chunks):
+                    logit_tiles[index + 1] = load_logits(*chunks[index + 1])
+                fold_rows(nc.gpsimd, e)
+            if dy == 5:
+                fold_columns(nc.gpsimd, e)
 
-        def end_waiting():
-            if state["waiting"]:
-                finish(*state["waiting"])
-
-        def step_a():
-            ready[1] = project(1, quantised)
-            softmax(1, second_logits)
-            state["lt"] = load_logits(1, 0)
-
-        def step_b():
-            quantised[0:2] = [quantised_weights(1, cp) for cp in range(2)]
-
-        def step_c():
-            quantised[2:4] = [quantised_weights(1, cp) for cp in range(2, 4)]
-
-        def step_d():
-            softmax(2, state["lt"])
-            state["lt"] = load_logits(1, 1)
-            ready[2] = project(0, quantised)
-
-        def step_e():
-            ready[3] = project(1, quantised)
-            softmax(3, state["lt"])
-
-        plans = [
-            {0: step_a, 2: step_b, 4: step_c},
-            {0: end_waiting, 1: step_d},
-            {0: end_waiting, 1: step_e},
-            {0: end_waiting},
-        ]
         for index, (hh, t) in enumerate(chunks):
-            banks, spread = ready[index]
-            sums = window_sum(weights[index % 2], banks, spread, plans[index])
-            state["waiting"] = (hh, t, sums, turned_sums[index])
-        end_waiting()
+
+            def between(dy):
+                if dy == 0 and waiting:
+                    finish(*waiting.pop())
+                if index + 1 < len(chunks):
+                    prepare(index + 1, dy)
+                    if dy == 1:
+                        ready[index + 1] = project(chunks[index + 1][1], quantised[chunks[index + 1][0]])
+                if index == 0 and 2 <= dy < 6:
+                    quantised.setdefault(1, []).append(quantised_weights(1, dy - 2))
+
+            sums = window_sum(weights[index % 2], *ready[index], between)
+            waiting.append((hh, t, sums, turned_sums[index]))
+        finish(*waiting.pop())

@@ -19,7 +19,10 @@ REACH = TAPS // 2
 SHARE = 8
 HALF = SHARE // 2
 SPARE = 2
-GPSIMD_DX = (3,)
+OWN_DX = REACH
+OWN_ORDER = (3, 0, 1, 2, 4, 5, 6)
+STRIDE = 52
+BANKS = {"x3": 4, "acc": 2, "aux": 2}
 FLOPS = 2 * 2048 * 2048 * 256 + 2 * 4 * 2048 * 64 * 49
 
 
@@ -39,6 +42,7 @@ def inside(d):
 def tile_sam_pb_kernel(tc, logits, x, w3c, b3c, out):
     nc = tc.nc
     with ExitStack() as stack:
+        stack.enter_context(tc.manual_schedule())
         keep = stack.enter_context(tc.tile_pool(name="keep", bufs=1))
         loads = stack.enter_context(tc.tile_pool(name="loads", bufs=2))
         stream = stack.enter_context(tc.tile_pool(name="stream", bufs=2))
@@ -47,7 +51,14 @@ def tile_sam_pb_kernel(tc, logits, x, w3c, b3c, out):
         ident = keep.tile([P, P], F32)
         make_identity(nc, ident[:])
 
-        weights = [keep.tile([P, TAPS * TAPS, SPOTS, 2], F32, name="weights%d" % r) for r in range(2)]
+        weights = [keep.tile([P, 2 * SPOTS * STRIDE], F32, name="weights%d" % r) for r in range(2)]
+
+        def by_tap(e):
+            return e[:, 0 : TAPS * TAPS * 2 * SPOTS].rearrange("p (dy dx i s) -> p dy dx i s", dy=TAPS, dx=TAPS, i=SIDE)
+
+        def by_place(e):
+            places = e[:].rearrange("p (i s l) -> p i s l", i=SIDE, l=STRIDE)[:, :, :, 0 : TAPS * TAPS]
+            return places.rearrange("p i s (dy dx) -> p dy dx i s", dx=TAPS)
 
         def load_logits(hh, t):
             lt = loads.tile([P, 2, TAPS * TAPS, SPOTS], BF16)
@@ -56,7 +67,8 @@ def tile_sam_pb_kernel(tc, logits, x, w3c, b3c, out):
             return lt
 
         def largest(lt):
-            top = loads.tile([P, 2, 24, SPOTS], BF16)
+            top = keep.tile([P, 2, 24, SPOTS], BF16)
+            most = loads.tile([P, 2, 1, SPOTS], BF16)
             nc.vector.tensor_tensor(out=top[:], in0=lt[:, :, 0:24, :], in1=lt[:, :, 24:48, :], op=ALU.max)
             width = 24
             while width > 1:
@@ -69,20 +81,31 @@ def tile_sam_pb_kernel(tc, logits, x, w3c, b3c, out):
                 )
                 width -= half
             nc.vector.tensor_tensor(
-                out=top[:, :, 0:1, :], in0=top[:, :, 0:1, :], in1=lt[:, :, 48:49, :], op=ALU.max
+                out=most[:], in0=top[:, :, 0:1, :], in1=lt[:, :, 48:49, :], op=ALU.max
             )
-            return top
+            return most
 
-        def shifted_exponentials(engine, lt, top, e, part):
+        def shifted_exponentials(lt, most, e, part):
             count = part.stop - part.start
-            engine.tensor_tensor(
-                out=e[:, part],
+            some = e[:, part.start * 2 * SPOTS : part.stop * 2 * SPOTS]
+            nc.vector.tensor_tensor(
+                out=some.rearrange("p (l n gl) -> p l n gl", l=count, gl=2),
                 in0=lt[:, :, part].rearrange("p gl l n -> p l n gl"),
-                in1=top[:, :, 0].rearrange("p gl n -> p n gl").unsqueeze(1).to_broadcast([P, count, SPOTS, 2]),
+                in1=most[:, :, 0].rearrange("p gl n -> p n gl").unsqueeze(1).to_broadcast([P, count, SPOTS, 2]),
                 op=ALU.subtract,
             )
-            flat = e[:, part].rearrange("p l n gl -> p (l n gl)")
-            nc.scalar.activation(out=flat, in_=flat, func=ACT.Exp)
+            nc.scalar.activation(out=some, in_=some, func=ACT.Exp)
+
+        def place_exponentials(lt, shift, e, total, places):
+            for place in places:
+                n, gl = divmod(place, 2)
+                nc.scalar.activation(
+                    out=e[:, place * STRIDE : place * STRIDE + TAPS * TAPS],
+                    in_=lt[:, gl, :, n],
+                    func=ACT.Exp,
+                    bias=shift[:, gl, n : n + 1],
+                    accum_out=total[:, place : place + 1],
+                )
 
         folds = []
         for s in range(SIDE):
@@ -91,19 +114,50 @@ def tile_sam_pb_kernel(tc, logits, x, w3c, b3c, out):
                 if mirrored(u) != u:
                     folds.append((s, d, mirrored(u) - s + REACH))
 
-        def fold_rows(engine, e):
-            taps = e[:].rearrange("p (dy dx) (i j) gl -> p dy dx i (j gl)", dx=TAPS, j=SIDE)
+        def fold_rows(engine, taps, order):
             for i, dy, twin_dy in folds:
-                twin = taps[:, twin_dy, :, i]
-                engine.tensor_tensor(out=twin, in0=twin, in1=taps[:, dy, :, i], op=ALU.add)
+                twin, own = [taps[:, d, :, i].rearrange("p dx s -> p " + order) for d in (twin_dy, dy)]
+                engine.tensor_tensor(out=twin, in0=twin, in1=own, op=ALU.add)
 
-        def fold_columns(engine, e):
-            taps = e[:].rearrange("p (dy dx) (i j) gl -> p dy dx i j gl", dx=TAPS, j=SIDE)
+        def fold_columns(engine, taps, lines, order):
             for j, dx, twin_dx in folds:
-                twin = taps[:, :, twin_dx, :, j]
-                engine.tensor_tensor(out=twin, in0=twin, in1=taps[:, :, dx, :, j], op=ALU.add)
+                twin, own = [
+                    taps[:, :, d, lines, 2 * j : 2 * j + 2].rearrange("p dy i gl -> p " + order) for d in (twin_dx, dx)
+                ]
+                engine.tensor_tensor(out=twin, in0=twin, in1=own, op=ALU.add)
 
-        first_logits = load_logits(0, 0)
+        w_view = w3c.rearrange("(hh k c) q -> hh k c q", hh=2, k=P, c=SHARE)
+
+        def load_channel(hh, c):
+            w_sb = stream.tile([P, 2048], BF16, bufs=5)
+            nc.sync.dma_start(out=w_sb[:], in_=w_view[hh][:, c, :])
+            return w_sb
+
+        def turned_channel(w_sb, copy, tag):
+            words = w_sb[:].bitcast(F32)
+            grouped_w = stream.tile([P, 4, P, 4], BF16, align_bytes=64, bufs=3)
+            for pair in range(2):
+                wt = psum.tile([P, 2, 2, P], F32, tag=tag, bufs=BANKS[tag])
+                for gl in range(2):
+                    for u in range(2):
+                        q = 2 * (2 * pair + gl) + u
+                        nc.tensor.transpose(wt[:, gl, u, :], words[:, q * P : (q + 1) * P], ident[:])
+                some = grouped_w[:, 2 * pair : 2 * pair + 2].rearrange("p g o f -> p g (o f)").bitcast(F32)
+                copy(out=some.rearrange("p g (o u) -> p g o u", u=2), in_=wt[:].rearrange("p g u o -> p g o u"))
+            return grouped_w
+
+        def quantised_channel(grouped_w):
+            codes_w = stream.tile([P, 4, P], U32, align_bytes=64, bufs=SHARE)
+            scales_w = stream.tile([P, 4, P], U8, align_bytes=64, bufs=SHARE)
+            nc.vector.quantize_mx(
+                out=codes_w[:].rearrange("p g o -> p (g o)").bitcast(FP8X4),
+                scales=scales_w[:].rearrange("p g o -> p (g o)"),
+                in_=grouped_w[:].rearrange("p g o f -> p (g o f)"),
+            )
+            return codes_w, scales_w
+
+        logit_tiles = {0: load_logits(0, 0)}
+        tops = {0: largest(logit_tiles[0])}
         bias_bf = keep.tile([P, 2, SHARE], BF16)
         bias = keep.tile([P, 2, SHARE], F32)
 
@@ -115,73 +169,53 @@ def tile_sam_pb_kernel(tc, logits, x, w3c, b3c, out):
                 out=raw_x[:],
                 in_=x.rearrange("b (g u p e) i j -> p (b g u) (e i j)", g=4, u=2, p=P, e=2),
             )
+            channels = [load_channel(0, c) for c in range(5)]
+            logit_tiles[1] = load_logits(0, 1)
             nc.sync.dma_start(out=bias_bf[:], in_=b3c.rearrange("(hh k c) -> k hh c", hh=2, k=P, c=SHARE))
+            grouped = [turned_channel(channels[c], nc.scalar.copy, "aux") for c in range(2)]
+            for part in (slice(0, 21), slice(21, 49)):
+                shifted_exponentials(logit_tiles[0], tops[0], weights[0], part)
             grouped_x = once.tile([P, 4, 2, SPOTS, 2, 4], BF16, align_bytes=64)
             raw_view = raw_x[:].rearrange("p (t gl g u) (e n) -> p g t n gl (u e)", t=2, gl=2, g=4, u=2, e=2)
             for g in range(4):
                 for t in range(2):
-                    nc.scalar.copy(out=grouped_x[:, g, t], in_=raw_view[:, g, t])
+                    nc.vector.tensor_copy(out=grouped_x[:, g, t], in_=raw_view[:, g, t])
             nc.vector.quantize_mx(
                 out=codes_x[:].rearrange("p g n -> p (g n)").bitcast(FP8X4),
                 scales=scales_x[:].rearrange("p g n -> p (g n)"),
                 in_=grouped_x[:].rearrange("p g t n gl f -> p (g t n gl f)"),
             )
-        nc.scalar.copy(out=bias[:], in_=bias_bf[:])
         flow = stack.enter_context(tc.tile_pool(name="flow", bufs=1))
         ends = stack.enter_context(tc.tile_pool(name="ends", bufs=2))
 
-        products = []
+        products = {}
         for dx in range(TAPS):
+            if dx == OWN_DX:
+                continue
             first, count = inside(dx)
-            spares = [flow.tile([P, SIDE, SIDE, 2 * SHARE], F32, name="product%d_%d" % (dx, s)) for s in range(SPARE)]
-            for spare in spares:
+            products[dx] = [
+                flow.tile([P, SIDE, SIDE, 2 * SHARE], F32, name="product%d_%d" % (dx, s)) for s in range(SPARE)
+            ]
+            for spare in products[dx]:
                 if first > 0:
                     nc.gpsimd.memset(spare[:, :, 0:first, :], 0.0)
                 if first + count < SIDE:
                     nc.gpsimd.memset(spare[:, :, first + count : SIDE, :], 0.0)
-            products.append(spares)
-
-        w_view = w3c.rearrange("(hh k c) q -> hh k c q", hh=2, k=P, c=SHARE)
-
-        def quantised_weights(hh, cp):
-            w_sb = stream.tile([P, 2, 2048], BF16)
-            nc.sync.dma_start(out=w_sb[:], in_=w_view[hh][:, 2 * cp : 2 * cp + 2, :])
-            grouped_w = stream.tile([P, 4, 256, 4], BF16, align_bytes=64)
-            for g in range(4):
-                wt = psum.tile([P, 2, 256], F32, tag="aux")
-                for u in range(2):
-                    for cl in range(2):
-                        words = w_sb[:, cl, :].bitcast(F32)
-                        nc.tensor.transpose(
-                            wt[:, u, cl * P : (cl + 1) * P],
-                            words[:, (2 * g + u) * P : (2 * g + u + 1) * P],
-                            ident[:],
-                        )
-                nc.scalar.copy(out=grouped_w[:, g].bitcast(F32), in_=wt[:].rearrange("p u o -> p o u"))
-            codes_w = stream.tile([P, 4, 256], U32, align_bytes=64, bufs=4)
-            scales_w = stream.tile([P, 4, 256], U8, align_bytes=64, bufs=4)
-            nc.vector.quantize_mx(
-                out=codes_w[:].rearrange("p g o -> p (g o)").bitcast(FP8X4),
-                scales=scales_w[:].rearrange("p g o -> p (g o)"),
-                in_=grouped_w[:].rearrange("p g o f -> p (g o f)"),
-            )
-            return codes_w, scales_w
 
         def project(t, quantised):
             spread = ends.tile([P, SPOTS * 2, SHARE], F32)
             banks = []
             columns = slice(t * P, (t + 1) * P)
             for half in range(2):
-                bank = psum.tile([P, HALF, P], F32, tag="x3", bufs=4)
+                bank = psum.tile([P, HALF, P], F32, tag="x3", bufs=BANKS["x3"])
                 for r in range(HALF):
                     c = half * HALF + r
-                    codes_w, scales_w = quantised[c // 2]
-                    own = slice((c % 2) * P, (c % 2 + 1) * P)
+                    codes_w, scales_w = quantised[c]
                     for g in range(4):
                         nc.tensor.matmul_mx(
                             out=bank[:, r, :],
-                            lhsT=codes_w[:, g, own].bitcast(FP8X4),
-                            lhsT_scale=scales_w[:, g, own],
+                            lhsT=codes_w[:, g, :].bitcast(FP8X4),
+                            lhsT_scale=scales_w[:, g, :],
                             rhs=codes_x[:, g, columns].bitcast(FP8X4),
                             rhs_scale=scales_x[:, g, columns],
                             start=(g == 0),
@@ -200,24 +234,26 @@ def tile_sam_pb_kernel(tc, logits, x, w3c, b3c, out):
             for tap in range(TAPS * TAPS):
                 nc.tensor.matmul(
                     out=both[:],
-                    lhsT=e[:, tap].rearrange("p n gl -> p (n gl)"),
+                    lhsT=e[:, tap * 2 * SPOTS : (tap + 1) * 2 * SPOTS],
                     rhs=ident[:],
                     is_transpose=True,
                     start=(tap == 0),
                     stop=(tap == TAPS * TAPS - 1),
                 )
-            turned_sum = ends.tile([P, P], F32, bufs=3)
+            turned_sum = ends.tile([P, P], F32)
             nc.scalar.copy(out=turned_sum[:], in_=both[:])
-            return turned_sum
+            again = psum.tile([P, P], F32, tag="aux")
+            nc.tensor.transpose(again[:], turned_sum[:], ident[:])
+            total = ends.tile([P, P], F32)
+            nc.scalar.copy(out=total[:], in_=again[:])
+            return total
 
-        def finish(hh, t, sums, turned_sum):
+        def finish(hh, t, sums, total):
             turned = ends.tile([P, SIDE, P], F32)
             for bank in range(2):
                 nc.scalar.copy(
                     out=turned[:].rearrange("p (h bank) k -> p bank h k", bank=2)[:, bank], in_=sums[bank][:]
                 )
-            total = psum.tile([P, P], F32, tag="aux")
-            nc.tensor.transpose(total[:], turned_sum[:], ident[:])
             rec = ends.tile([P, SIDE, SIDE, 2], F32)
             nc.vector.reciprocal(out=rec[:].rearrange("p i j gl -> p (i j gl)"), in_=total[:])
             result = ends.tile([P, 2, SHARE, SIDE, SIDE], F32)
@@ -243,22 +279,20 @@ def tile_sam_pb_kernel(tc, logits, x, w3c, b3c, out):
                     out=out_view[hh, :, 2 * t + gl], in_=result[:, gl].rearrange("p c i j -> p c (i j)")
                 )
 
-        def window_sum(e, banks, spread, between):
-            taps = e[:].rearrange("p (dy dx) (i j) gl -> p dy dx i (j gl)", dx=TAPS, j=SIDE)
+        def window_sum(taps, banks, spread, between):
             sources = [bank[:].rearrange("p c (i s) -> p i s c", i=SIDE) for bank in banks]
             spread_rows = spread[:].rearrange("p (i s) c -> p i s c", i=SIDE)
             sums = [psum.tile([P, SIDE // 2, P], F32, tag="acc", name="sums%d" % bank) for bank in range(2)]
             opened = set()
-            left = [sum(1 for dy in range(TAPS) for i in range(SIDE) if 0 <= i + dy - REACH < SIDE and i % 2 == b) * TAPS for b in range(2)]
+            left = [len(products) * sum(inside(dy)[1] for dy in range(TAPS)) // 2 + SIDE // 2] * 2
 
-            def add(dy, product):
-                first, count = inside(dy)
-                for i in range(first, first + count):
+            def add(lines, product):
+                for i in range(lines.start, lines.stop):
                     bank = i % 2
                     left[bank] -= 1
                     nc.tensor.matmul(
                         out=sums[bank][:, i // 2, :],
-                        lhsT=product[:, i].rearrange("p j s -> p (j s)"),
+                        lhsT=product[:, i],
                         rhs=ident[:],
                         is_transpose=True,
                         start=(bank not in opened),
@@ -266,28 +300,31 @@ def tile_sam_pb_kernel(tc, logits, x, w3c, b3c, out):
                     )
                     opened.add(bank)
 
-            late = []
+            own_sum = flow.tile([P, SIDE, SIDE * 2, SHARE], F32, bufs=2)
+
+            def own_row(dy):
+                i0, rows = inside(dy)
+                lines = slice(i0, i0 + rows)
+                target = own_sum
+                if dy != OWN_ORDER[0]:
+                    target = flow.tile([P, SIDE, SIDE * 2, SHARE], F32, bufs=2, name="own_product")
+                nc.gpsimd.tensor_tensor(
+                    out=target[:, lines],
+                    in0=spread_rows[:, i0 + dy - REACH : i0 + dy - REACH + rows],
+                    in1=taps[:, dy, OWN_DX, lines].unsqueeze(3).to_broadcast([P, rows, 2 * SIDE, SHARE]),
+                    op=ALU.mult,
+                )
+                if dy != OWN_ORDER[0]:
+                    nc.gpsimd.tensor_tensor(
+                        out=own_sum[:, lines], in0=own_sum[:, lines], in1=target[:, lines], op=ALU.add
+                    )
+
             for dy in range(TAPS):
                 i0, rows = inside(dy)
                 lines = slice(i0, i0 + rows)
                 source_lines = slice(i0 + dy - REACH, i0 + dy - REACH + rows)
-                new_late = []
-                for dx in GPSIMD_DX:
-                    j0, columns = inside(dx)
-                    product = products[dx][dy % SPARE]
-                    s0, s1 = 2 * (j0 + dx - REACH), 2 * (j0 + dx - REACH + columns)
-                    nc.gpsimd.tensor_tensor(
-                        out=product[:, lines, j0 : j0 + columns].rearrange("p i j (gl c) -> p i (j gl) c", gl=2),
-                        in0=spread_rows[:, source_lines, s0:s1],
-                        in1=taps[:, dy, dx, lines, 2 * j0 : 2 * (j0 + columns)]
-                        .unsqueeze(3)
-                        .to_broadcast([P, rows, 2 * columns, SHARE]),
-                        op=ALU.mult,
-                    )
-                    new_late.append((dy, product))
-                for dx in range(TAPS):
-                    if dx in GPSIMD_DX:
-                        continue
+                own_row(OWN_ORDER[dy])
+                for dx in products:
                     j0, columns = inside(dx)
                     product = products[dx][dy % SPARE]
                     s0, s1 = 2 * (j0 + dx - REACH), 2 * (j0 + dx - REACH + columns)
@@ -302,45 +339,51 @@ def tile_sam_pb_kernel(tc, logits, x, w3c, b3c, out):
                             .to_broadcast([P, rows, 2 * columns, HALF]),
                             op=ALU.mult,
                         )
-                    add(dy, product)
-                for old in late:
-                    add(*old)
-                late = new_late
+                    add(lines, product[:].rearrange("p i j s -> p i (j s)"))
                 between(dy)
-            for old in late:
-                add(*old)
+            add(slice(0, SIDE), own_sum[:].rearrange("p i s c -> p i (s c)"))
             return sums
 
         chunks = [(hh, t) for hh in range(2) for t in range(2)]
-        parts = [slice(TAPS * dy, TAPS * dy + TAPS) for dy in range(TAPS)]
-        turned_sums, ready, quantised, logit_tiles, tops = {}, {}, {}, {0: first_logits}, {}
-        waiting = []
-
-        quantised[0] = [quantised_weights(0, 0)]
-        tops[0] = largest(first_logits)
-        for part in (slice(0, 25), slice(25, 49)):
-            shifted_exponentials(nc.vector, first_logits, tops[0], weights[0], part)
-        quantised[0].extend(quantised_weights(0, cp) for cp in range(1, 4))
-        logit_tiles[1] = load_logits(0, 1)
-        turned_sums[0] = numerator_sums(weights[0])
-        fold_rows(nc.vector, weights[0])
-        fold_columns(nc.vector, weights[0])
+        totals, ready, quantised, waiting = {}, {}, {0: [], 1: []}, []
+        for c in range(5, SHARE):
+            channels.append(load_channel(0, c))
+        quantised[0].extend(quantised_channel(grouped.pop(0)) for c in range(2))
+        for c in range(2, SHARE):
+            copy, tag = (nc.scalar.copy, "acc") if c % 2 else (nc.vector.tensor_copy, "x3")
+            quantised[0].append(quantised_channel(turned_channel(channels[c], copy, tag)))
+            if c == 3:
+                totals[0] = numerator_sums(weights[0])
+        fold_rows(nc.vector, by_tap(weights[0]), "dx s")
+        fold_columns(nc.vector, by_tap(weights[0]), slice(0, SIDE), "dy i gl")
+        nc.scalar.copy(out=bias[:], in_=bias_bf[:])
         ready[0] = project(0, quantised[0])
+        channels = [load_channel(1, c) for c in range(5)]
+
+        places = [n * 2 + gl for i in (0, 1, 2, 5, 6, 7, 3, 4) for n in range(SIDE * i, SIDE * i + SIDE) for gl in range(2)]
+        stretch = 2 * SPOTS // 4
+        shifts = {}
 
         def prepare(index, dy):
             e = weights[index % 2]
             if dy == 0:
-                tops[index] = largest(logit_tiles[index])
+                most = largest(logit_tiles[index])
+                shift = loads.tile([P, 2, SPOTS], F32)
+                nc.vector.tensor_scalar(out=shift[:], in0=most[:, :, 0], scalar1=-1.0, scalar2=None, op0=ALU.mult)
+                total = ends.tile([P, P], F32)
+                shifts[index], totals[index] = shift, total
             if dy < 4:
-                for part in parts[2 * dy : 2 * dy + 2]:
-                    shifted_exponentials(nc.gpsimd, logit_tiles[index], tops[index], e, part)
+                some = places[stretch * dy : stretch * dy + stretch]
+                place_exponentials(logit_tiles[index], shifts[index], e, totals[index], some)
             if dy == 4:
-                turned_sums[index] = numerator_sums(e)
                 if index + 1 < len(chunks):
                     logit_tiles[index + 1] = load_logits(*chunks[index + 1])
-                fold_rows(nc.gpsimd, e)
+                fold_rows(nc.gpsimd, by_place(e), "s dx")
             if dy == 5:
-                fold_columns(nc.gpsimd, e)
+                for lines in (slice(0, 3), slice(5, 8)):
+                    fold_columns(nc.gpsimd, by_place(e), lines, "i gl dy")
+            if dy == 6:
+                fold_columns(nc.gpsimd, by_place(e), slice(3, 5), "i gl dy")
 
         for index, (hh, t) in enumerate(chunks):
 
@@ -348,12 +391,18 @@ def tile_sam_pb_kernel(tc, logits, x, w3c, b3c, out):
                 if dy == 0 and waiting:
                     finish(*waiting.pop())
                 if index + 1 < len(chunks):
-                    prepare(index + 1, dy)
-                    if dy == 1:
+                    if dy == (0 if index == 0 else 3):
                         ready[index + 1] = project(chunks[index + 1][1], quantised[chunks[index + 1][0]])
-                if index == 0 and 2 <= dy < 6:
-                    quantised.setdefault(1, []).append(quantised_weights(1, dy - 2))
+                    prepare(index + 1, dy)
+                step = TAPS * index + dy - 1
+                if 1 <= step <= SHARE:
+                    quantised[1].append(quantised_channel(grouped.pop(0)))
+                if 0 <= step < SHARE:
+                    if step + 5 < SHARE:
+                        channels.append(load_channel(1, step + 5))
+                    grouped.append(turned_channel(channels[step], nc.scalar.copy, "aux"))
 
-            sums = window_sum(weights[index % 2], *ready[index], between)
-            waiting.append((hh, t, sums, turned_sums[index]))
+            taps = by_place(weights[index % 2]) if index else by_tap(weights[0])
+            sums = window_sum(taps, *ready[index], between)
+            waiting.append((hh, t, sums, totals[index]))
         finish(*waiting.pop())

@@ -20,7 +20,8 @@ SHARE = 8
 HALF = SHARE // 2
 SPARE = 2
 OWN_DX = REACH
-OWN_ORDER = (3, 0, 1, 2, 4, 5, 6)
+AHEAD = 3
+LAG = 2
 STRIDE = 52
 BANKS = {"x3": 4, "acc": 2, "aux": 2}
 FLOPS = 2 * 2048 * 2048 * 256 + 2 * 4 * 2048 * 64 * 49
@@ -51,7 +52,7 @@ def tile_sam_pb_kernel(tc, logits, x, w3c, b3c, out):
         ident = keep.tile([P, P], F32)
         make_identity(nc, ident[:])
 
-        weights = [keep.tile([P, 2 * SPOTS * STRIDE], F32, name="weights%d" % r) for r in range(2)]
+        weights = [keep.tile([P, 2 * SPOTS * STRIDE], F32, name="weights%d" % r) for r in range(3)]
 
         def by_tap(e):
             return e[:, 0 : TAPS * TAPS * 2 * SPOTS].rearrange("p (dy dx i s) -> p dy dx i s", dy=TAPS, dx=TAPS, i=SIDE)
@@ -129,13 +130,13 @@ def tile_sam_pb_kernel(tc, logits, x, w3c, b3c, out):
         w_view = w3c.rearrange("(hh k c) q -> hh k c q", hh=2, k=P, c=SHARE)
 
         def load_channel(hh, c):
-            w_sb = stream.tile([P, 2048], BF16, bufs=5)
+            w_sb = stream.tile([P, 2048], BF16, bufs=AHEAD)
             nc.sync.dma_start(out=w_sb[:], in_=w_view[hh][:, c, :])
             return w_sb
 
         def turned_channel(w_sb, copy, tag):
             words = w_sb[:].bitcast(F32)
-            grouped_w = stream.tile([P, 4, P, 4], BF16, align_bytes=64, bufs=3)
+            grouped_w = stream.tile([P, 4, P, 4], BF16, align_bytes=64)
             for pair in range(2):
                 wt = psum.tile([P, 2, 2, P], F32, tag=tag, bufs=BANKS[tag])
                 for gl in range(2):
@@ -169,7 +170,7 @@ def tile_sam_pb_kernel(tc, logits, x, w3c, b3c, out):
                 out=raw_x[:],
                 in_=x.rearrange("b (g u p e) i j -> p (b g u) (e i j)", g=4, u=2, p=P, e=2),
             )
-            channels = [load_channel(0, c) for c in range(5)]
+            channels = [load_channel(0, c) for c in range(AHEAD)]
             logit_tiles[1] = load_logits(0, 1)
             nc.sync.dma_start(out=bias_bf[:], in_=b3c.rearrange("(hh k c) -> k hh c", hh=2, k=P, c=SHARE))
             grouped = [turned_channel(channels[c], nc.scalar.copy, "aux") for c in range(2)]
@@ -190,11 +191,10 @@ def tile_sam_pb_kernel(tc, logits, x, w3c, b3c, out):
 
         products = {}
         for dx in range(TAPS):
-            if dx == OWN_DX:
-                continue
             first, count = inside(dx)
             products[dx] = [
-                flow.tile([P, SIDE, SIDE, 2 * SHARE], F32, name="product%d_%d" % (dx, s)) for s in range(SPARE)
+                flow.tile([P, SIDE, SIDE, 2 * SHARE], F32, name="product%d_%d" % (dx, s))
+                for s in range(LAG + 1 if dx == OWN_DX else SPARE)
             ]
             for spare in products[dx]:
                 if first > 0:
@@ -244,19 +244,19 @@ def tile_sam_pb_kernel(tc, logits, x, w3c, b3c, out):
             nc.scalar.copy(out=turned_sum[:], in_=both[:])
             again = psum.tile([P, P], F32, tag="aux")
             nc.tensor.transpose(again[:], turned_sum[:], ident[:])
-            total = ends.tile([P, P], F32)
+            total = ends.tile([P, P], F32, bufs=3)
             nc.scalar.copy(out=total[:], in_=again[:])
             return total
 
         def finish(hh, t, sums, total):
-            turned = ends.tile([P, SIDE, P], F32)
+            turned = ends.tile([P, SIDE, P], F32, bufs=1)
             for bank in range(2):
                 nc.scalar.copy(
                     out=turned[:].rearrange("p (h bank) k -> p bank h k", bank=2)[:, bank], in_=sums[bank][:]
                 )
             rec = ends.tile([P, SIDE, SIDE, 2], F32)
             nc.vector.reciprocal(out=rec[:].rearrange("p i j gl -> p (i j gl)"), in_=total[:])
-            result = ends.tile([P, 2, SHARE, SIDE, SIDE], F32)
+            result = ends.tile([P, 2, SHARE, SIDE, SIDE], F32, bufs=1)
             for half in range(2):
                 some = slice(4 * half, 4 * half + 4)
                 back = psum.tile([P, 4, SIDE, 2, SHARE], F32, tag="aux")
@@ -279,12 +279,12 @@ def tile_sam_pb_kernel(tc, logits, x, w3c, b3c, out):
                     out=out_view[hh, :, 2 * t + gl], in_=result[:, gl].rearrange("p c i j -> p c (i j)")
                 )
 
-        def window_sum(taps, banks, spread, between):
+        def window_sum(index, taps, banks, spread, between):
             sources = [bank[:].rearrange("p c (i s) -> p i s c", i=SIDE) for bank in banks]
             spread_rows = spread[:].rearrange("p (i s) c -> p i s c", i=SIDE)
             sums = [psum.tile([P, SIDE // 2, P], F32, tag="acc", name="sums%d" % bank) for bank in range(2)]
             opened = set()
-            left = [len(products) * sum(inside(dy)[1] for dy in range(TAPS)) // 2 + SIDE // 2] * 2
+            left = [TAPS * sum(inside(dy)[1] for dy in range(TAPS)) // 2] * 2
 
             def add(lines, product):
                 for i in range(lines.start, lines.stop):
@@ -292,7 +292,7 @@ def tile_sam_pb_kernel(tc, logits, x, w3c, b3c, out):
                     left[bank] -= 1
                     nc.tensor.matmul(
                         out=sums[bank][:, i // 2, :],
-                        lhsT=product[:, i],
+                        lhsT=product[:, i].rearrange("p j s -> p (j s)"),
                         rhs=ident[:],
                         is_transpose=True,
                         start=(bank not in opened),
@@ -300,33 +300,24 @@ def tile_sam_pb_kernel(tc, logits, x, w3c, b3c, out):
                     )
                     opened.add(bank)
 
-            own_sum = flow.tile([P, SIDE, SIDE * 2, SHARE], F32, bufs=2)
-
-            def own_row(dy):
-                i0, rows = inside(dy)
-                lines = slice(i0, i0 + rows)
-                target = own_sum
-                if dy != OWN_ORDER[0]:
-                    target = flow.tile([P, SIDE, SIDE * 2, SHARE], F32, bufs=2, name="own_product")
-                nc.gpsimd.tensor_tensor(
-                    out=target[:, lines],
-                    in0=spread_rows[:, i0 + dy - REACH : i0 + dy - REACH + rows],
-                    in1=taps[:, dy, OWN_DX, lines].unsqueeze(3).to_broadcast([P, rows, 2 * SIDE, SHARE]),
-                    op=ALU.mult,
-                )
-                if dy != OWN_ORDER[0]:
-                    nc.gpsimd.tensor_tensor(
-                        out=own_sum[:, lines], in0=own_sum[:, lines], in1=target[:, lines], op=ALU.add
-                    )
-
+            late = []
             for dy in range(TAPS):
                 i0, rows = inside(dy)
                 lines = slice(i0, i0 + rows)
                 source_lines = slice(i0 + dy - REACH, i0 + dy - REACH + rows)
-                own_row(OWN_ORDER[dy])
-                for dx in products:
+                turn = TAPS * index + dy
+                product = products[OWN_DX][turn % (LAG + 1)]
+                nc.gpsimd.tensor_tensor(
+                    out=product[:, lines].rearrange("p i j (gl c) -> p i (j gl) c", gl=2),
+                    in0=spread_rows[:, source_lines],
+                    in1=taps[:, dy, OWN_DX, lines].unsqueeze(3).to_broadcast([P, rows, 2 * SIDE, SHARE]),
+                    op=ALU.mult,
+                )
+                late.append((lines, product))
+                own = [dx for dx in range(TAPS) if dx != OWN_DX]
+                for dx in own[::-1] if turn // SPARE % 2 else own:
                     j0, columns = inside(dx)
-                    product = products[dx][dy % SPARE]
+                    product = products[dx][turn % SPARE]
                     s0, s1 = 2 * (j0 + dx - REACH), 2 * (j0 + dx - REACH + columns)
                     for half in range(2):
                         nc.vector.tensor_tensor(
@@ -339,14 +330,31 @@ def tile_sam_pb_kernel(tc, logits, x, w3c, b3c, out):
                             .to_broadcast([P, rows, 2 * columns, HALF]),
                             op=ALU.mult,
                         )
-                    add(lines, product[:].rearrange("p i j s -> p i (j s)"))
+                    add(lines, product)
+                if dy >= LAG:
+                    add(*late.pop(0))
                 between(dy)
-            add(slice(0, SIDE), own_sum[:].rearrange("p i s c -> p i (s c)"))
+            for some in late:
+                add(*some)
             return sums
 
         chunks = [(hh, t) for hh in range(2) for t in range(2)]
         totals, ready, quantised, waiting = {}, {}, {0: [], 1: []}, []
-        for c in range(5, SHARE):
+        shifts, done = {}, {}
+
+        def begin(index):
+            most = largest(logit_tiles[index])
+            shift = loads.tile([P, 2, SPOTS], F32)
+            nc.vector.tensor_scalar(out=shift[:], in0=most[:, :, 0], scalar1=-1.0, scalar2=None, op0=ALU.mult)
+            total = ends.tile([P, P], F32, bufs=3)
+            shifts[index], totals[index], done[index] = shift, total, 0
+
+        def advance(index, until):
+            some = range(done[index], until)
+            place_exponentials(logit_tiles[index], shifts[index], weights[index % 3], totals[index], some)
+            done[index] = until
+
+        for c in range(AHEAD, SHARE):
             channels.append(load_channel(0, c))
         quantised[0].extend(quantised_channel(grouped.pop(0)) for c in range(2))
         for c in range(2, SHARE):
@@ -354,36 +362,31 @@ def tile_sam_pb_kernel(tc, logits, x, w3c, b3c, out):
             quantised[0].append(quantised_channel(turned_channel(channels[c], copy, tag)))
             if c == 3:
                 totals[0] = numerator_sums(weights[0])
+        begin(1)
         fold_rows(nc.vector, by_tap(weights[0]), "dx s")
         fold_columns(nc.vector, by_tap(weights[0]), slice(0, SIDE), "dy i gl")
         nc.scalar.copy(out=bias[:], in_=bias_bf[:])
         ready[0] = project(0, quantised[0])
-        channels = [load_channel(1, c) for c in range(5)]
+        channels = [load_channel(1, c) for c in range(AHEAD)]
 
-        places = [n * 2 + gl for i in (0, 1, 2, 5, 6, 7, 3, 4) for n in range(SIDE * i, SIDE * i + SIDE) for gl in range(2)]
-        stretch = 2 * SPOTS // 4
-        shifts = {}
+        advance(1, 32)
 
         def prepare(index, dy):
-            e = weights[index % 2]
-            if dy == 0:
-                most = largest(logit_tiles[index])
-                shift = loads.tile([P, 2, SPOTS], F32)
-                nc.vector.tensor_scalar(out=shift[:], in0=most[:, :, 0], scalar1=-1.0, scalar2=None, op0=ALU.mult)
-                total = ends.tile([P, P], F32)
-                shifts[index], totals[index] = shift, total
-            if dy < 4:
-                some = places[stretch * dy : stretch * dy + stretch]
-                place_exponentials(logit_tiles[index], shifts[index], e, totals[index], some)
-            if dy == 4:
-                if index + 1 < len(chunks):
-                    logit_tiles[index + 1] = load_logits(*chunks[index + 1])
-                fold_rows(nc.gpsimd, by_place(e), "s dx")
-            if dy == 5:
-                for lines in (slice(0, 3), slice(5, 8)):
-                    fold_columns(nc.gpsimd, by_place(e), lines, "i gl dy")
-            if dy == 6:
-                fold_columns(nc.gpsimd, by_place(e), slice(3, 5), "i gl dy")
+            if index + 1 < len(chunks) and dy < 4:
+                start = 32 if index == 0 else 56
+                advance(index + 1, start + (2 * SPOTS - start) * (dy + 1) // 4)
+            if index + 2 < len(chunks) and dy == 2:
+                logit_tiles[index + 2] = load_logits(*chunks[index + 2])
+            if index + 2 < len(chunks) and dy >= 4:
+                if dy == 4:
+                    begin(index + 2)
+                advance(index + 2, (19, 38, 56)[dy - 4])
+            if index + 1 < len(chunks):
+                taps = by_place(weights[(index + 1) % 3])
+                if dy == 4:
+                    fold_rows(nc.gpsimd, taps, "s dx")
+                if dy == 5:
+                    fold_columns(nc.gpsimd, taps, slice(0, SIDE), "i gl dy")
 
         for index, (hh, t) in enumerate(chunks):
 
@@ -393,16 +396,16 @@ def tile_sam_pb_kernel(tc, logits, x, w3c, b3c, out):
                 if index + 1 < len(chunks):
                     if dy == (0 if index == 0 else 3):
                         ready[index + 1] = project(chunks[index + 1][1], quantised[chunks[index + 1][0]])
-                    prepare(index + 1, dy)
+                prepare(index, dy)
                 step = TAPS * index + dy - 1
                 if 1 <= step <= SHARE:
                     quantised[1].append(quantised_channel(grouped.pop(0)))
                 if 0 <= step < SHARE:
-                    if step + 5 < SHARE:
-                        channels.append(load_channel(1, step + 5))
+                    if step + AHEAD < SHARE:
+                        channels.append(load_channel(1, step + AHEAD))
                     grouped.append(turned_channel(channels[step], nc.scalar.copy, "aux"))
 
-            taps = by_place(weights[index % 2]) if index else by_tap(weights[0])
-            sums = window_sum(taps, *ready[index], between)
+            taps = by_place(weights[index % 3]) if index else by_tap(weights[0])
+            sums = window_sum(index, taps, *ready[index], between)
             waiting.append((hh, t, sums, totals[index]))
         finish(*waiting.pop())

@@ -21,6 +21,7 @@ HALF = SHARE // 2
 SPARE = 2
 OWN_DX = REACH
 AHEAD = 3
+HELP_DX = 2
 LAG = 2
 STRIDE = 52
 BANKS = {"x3": 4, "acc": 2, "aux": 2}
@@ -38,6 +39,11 @@ def mirrored(u):
 def inside(d):
     first = max(0, REACH - d)
     return first, min(SIDE, SIDE + REACH - d) - first
+
+
+def gpsimd_columns(index, dy):
+    helps = {0: (0, 1, 2), 3: range(TAPS)}.get(index, (0, 1, 6))
+    return (HELP_DX, OWN_DX) if dy in helps else (OWN_DX,)
 
 
 def tile_sam_pb_kernel(tc, logits, x, w3c, b3c, out):
@@ -97,7 +103,7 @@ def tile_sam_pb_kernel(tc, logits, x, w3c, b3c, out):
             )
             nc.scalar.activation(out=some, in_=some, func=ACT.Exp)
 
-        def place_exponentials(lt, shift, e, total, places):
+        def place_exponentials(lt, shift, e, places):
             for place in places:
                 n, gl = divmod(place, 2)
                 nc.scalar.activation(
@@ -105,7 +111,6 @@ def tile_sam_pb_kernel(tc, logits, x, w3c, b3c, out):
                     in_=lt[:, gl, :, n],
                     func=ACT.Exp,
                     bias=shift[:, gl, n : n + 1],
-                    accum_out=total[:, place : place + 1],
                 )
 
         folds = []
@@ -115,15 +120,15 @@ def tile_sam_pb_kernel(tc, logits, x, w3c, b3c, out):
                 if mirrored(u) != u:
                     folds.append((s, d, mirrored(u) - s + REACH))
 
-        def fold_rows(engine, taps, order):
-            for i, dy, twin_dy in folds:
+        def fold_rows(engine, taps, order, some=slice(0, 12)):
+            for i, dy, twin_dy in folds[some]:
                 twin, own = [taps[:, d, :, i].rearrange("p dx s -> p " + order) for d in (twin_dy, dy)]
                 engine.tensor_tensor(out=twin, in0=twin, in1=own, op=ALU.add)
 
-        def fold_columns(engine, taps, lines, order):
-            for j, dx, twin_dx in folds:
+        def fold_columns(engine, taps, order, some=slice(0, 12)):
+            for j, dx, twin_dx in folds[some]:
                 twin, own = [
-                    taps[:, :, d, lines, 2 * j : 2 * j + 2].rearrange("p dy i gl -> p " + order) for d in (twin_dx, dx)
+                    taps[:, :, d, :, 2 * j : 2 * j + 2].rearrange("p dy i gl -> p " + order) for d in (twin_dx, dx)
                 ]
                 engine.tensor_tensor(out=twin, in0=twin, in1=own, op=ALU.add)
 
@@ -134,7 +139,7 @@ def tile_sam_pb_kernel(tc, logits, x, w3c, b3c, out):
             nc.sync.dma_start(out=w_sb[:], in_=w_view[hh][:, c, :])
             return w_sb
 
-        def turned_channel(w_sb, copy, tag):
+        def turned_channel(w_sb, tag):
             words = w_sb[:].bitcast(F32)
             grouped_w = stream.tile([P, 4, P, 4], BF16, align_bytes=64)
             for pair in range(2):
@@ -144,7 +149,7 @@ def tile_sam_pb_kernel(tc, logits, x, w3c, b3c, out):
                         q = 2 * (2 * pair + gl) + u
                         nc.tensor.transpose(wt[:, gl, u, :], words[:, q * P : (q + 1) * P], ident[:])
                 some = grouped_w[:, 2 * pair : 2 * pair + 2].rearrange("p g o f -> p g (o f)").bitcast(F32)
-                copy(out=some.rearrange("p g (o u) -> p g o u", u=2), in_=wt[:].rearrange("p g u o -> p g o u"))
+                nc.scalar.copy(out=some.rearrange("p g (o u) -> p g o u", u=2), in_=wt[:].rearrange("p g u o -> p g o u"))
             return grouped_w
 
         def quantised_channel(grouped_w):
@@ -156,6 +161,17 @@ def tile_sam_pb_kernel(tc, logits, x, w3c, b3c, out):
                 in_=grouped_w[:].rearrange("p g o f -> p (g o f)"),
             )
             return codes_w, scales_w
+
+        def add_numerators(both, taps_of, part):
+            for tap in range(part.start, part.stop):
+                nc.tensor.matmul(
+                    out=both[:],
+                    lhsT=taps_of(tap),
+                    rhs=ident[:],
+                    is_transpose=True,
+                    start=(tap == 0),
+                    stop=(tap == TAPS * TAPS - 1),
+                )
 
         logit_tiles = {0: load_logits(0, 0)}
         tops = {0: largest(logit_tiles[0])}
@@ -173,14 +189,27 @@ def tile_sam_pb_kernel(tc, logits, x, w3c, b3c, out):
             channels = [load_channel(0, c) for c in range(AHEAD)]
             logit_tiles[1] = load_logits(0, 1)
             nc.sync.dma_start(out=bias_bf[:], in_=b3c.rearrange("(hh k c) -> k hh c", hh=2, k=P, c=SHARE))
-            grouped = [turned_channel(channels[c], nc.scalar.copy, "aux") for c in range(2)]
-            for part in (slice(0, 21), slice(21, 49)):
+            both = psum.tile([P, P], F32, tag="aux")
+            grouped = []
+            quantised = {0: [], 1: []}
+            for step, part in enumerate((slice(0, 12), slice(12, 24), slice(24, 36), slice(36, 49))):
                 shifted_exponentials(logit_tiles[0], tops[0], weights[0], part)
+                if step >= 2:
+                    quantised[0].append(quantised_channel(grouped.pop(0)))
+                if step == 3:
+                    channels.append(load_channel(0, 3))
+                grouped.append(turned_channel(channels[step], "acc" if step == 2 else "x3"))
+                add_numerators(both, lambda tap: weights[0][:, tap * 2 * SPOTS : (tap + 1) * 2 * SPOTS], part)
             grouped_x = once.tile([P, 4, 2, SPOTS, 2, 4], BF16, align_bytes=64)
             raw_view = raw_x[:].rearrange("p (t gl g u) (e n) -> p g t n gl (u e)", t=2, gl=2, g=4, u=2, e=2)
             for g in range(4):
                 for t in range(2):
                     nc.vector.tensor_copy(out=grouped_x[:, g, t], in_=raw_view[:, g, t])
+                if g % 2 == 1:
+                    for c in range(2):
+                        quantised[0].append(quantised_channel(grouped.pop(0)))
+                        channels.append(load_channel(0, len(channels)))
+                        grouped.append(turned_channel(channels[-1], "acc" if c else "x3"))
             nc.vector.quantize_mx(
                 out=codes_x[:].rearrange("p g n -> p (g n)").bitcast(FP8X4),
                 scales=scales_x[:].rearrange("p g n -> p (g n)"),
@@ -229,17 +258,7 @@ def tile_sam_pb_kernel(tc, logits, x, w3c, b3c, out):
 
         out_view = out.rearrange("b (hh k c) i j -> hh k b c (i j)", hh=2, k=P, c=SHARE)
 
-        def numerator_sums(e):
-            both = psum.tile([P, P], F32, tag="aux")
-            for tap in range(TAPS * TAPS):
-                nc.tensor.matmul(
-                    out=both[:],
-                    lhsT=e[:, tap * 2 * SPOTS : (tap + 1) * 2 * SPOTS],
-                    rhs=ident[:],
-                    is_transpose=True,
-                    start=(tap == 0),
-                    stop=(tap == TAPS * TAPS - 1),
-                )
+        def numerator_sums(both):
             turned_sum = ends.tile([P, P], F32)
             nc.scalar.copy(out=turned_sum[:], in_=both[:])
             again = psum.tile([P, P], F32, tag="aux")
@@ -248,33 +267,38 @@ def tile_sam_pb_kernel(tc, logits, x, w3c, b3c, out):
             nc.scalar.copy(out=total[:], in_=again[:])
             return total
 
-        def finish(hh, t, sums, total):
+        def turn_back(sums):
             turned = ends.tile([P, SIDE, P], F32, bufs=1)
             for bank in range(2):
                 nc.scalar.copy(
                     out=turned[:].rearrange("p (h bank) k -> p bank h k", bank=2)[:, bank], in_=sums[bank][:]
                 )
-            rec = ends.tile([P, SIDE, SIDE, 2], F32)
-            nc.vector.reciprocal(out=rec[:].rearrange("p i j gl -> p (i j gl)"), in_=total[:])
-            result = ends.tile([P, 2, SHARE, SIDE, SIDE], F32, bufs=1)
+            backs = []
             for half in range(2):
-                some = slice(4 * half, 4 * half + 4)
                 back = psum.tile([P, 4, SIDE, 2, SHARE], F32, tag="aux")
                 for r in range(4):
                     nc.tensor.transpose(
                         back[:, r].rearrange("p j gl c -> p (j gl c)"), turned[:, 4 * half + r, :], ident[:]
                     )
-                for gl in range(2):
+                backs.append(back)
+            return backs
+
+        def finish(hh, t, backs, total):
+            rec = ends.tile([P, SIDE, SIDE, 2], F32)
+            nc.vector.reciprocal(out=rec[:].rearrange("p i j gl -> p (i j gl)"), in_=total[:])
+            result = ends.tile([P, 2, SHARE, SIDE, SIDE], F32, bufs=1)
+            for gl in range(2):
+                for half in range(2):
+                    some = slice(4 * half, 4 * half + 4)
                     nc.vector.tensor_tensor(
                         out=result[:, gl, :, some, :],
-                        in0=back[:, :, :, gl].rearrange("p i j c -> p c i j"),
+                        in0=backs[half][:, :, :, gl].rearrange("p i j c -> p c i j"),
                         in1=rec[:, some, :, gl].unsqueeze(1).to_broadcast([P, SHARE, 4, SIDE]),
                         op=ALU.mult,
                     )
-            for c in range(SHARE):
-                lane = result[:, :, c].rearrange("p gl i j -> p gl (i j)")
-                nc.scalar.activation(out=lane, in_=lane, func=ACT.Identity, bias=bias[:, hh, c : c + 1])
-            for gl in range(2):
+                for c in range(SHARE):
+                    lane = result[:, gl, c].rearrange("p i j -> p (i j)")
+                    nc.scalar.activation(out=lane, in_=lane, func=ACT.Identity, bias=bias[:, hh, c : c + 1])
                 nc.sync.dma_start(
                     out=out_view[hh, :, 2 * t + gl], in_=result[:, gl].rearrange("p c i j -> p c (i j)")
                 )
@@ -301,20 +325,28 @@ def tile_sam_pb_kernel(tc, logits, x, w3c, b3c, out):
                     opened.add(bank)
 
             late = []
+            lags = {OWN_DX: LAG, HELP_DX: 1}
             for dy in range(TAPS):
                 i0, rows = inside(dy)
                 lines = slice(i0, i0 + rows)
                 source_lines = slice(i0 + dy - REACH, i0 + dy - REACH + rows)
                 turn = TAPS * index + dy
-                product = products[OWN_DX][turn % (LAG + 1)]
-                nc.gpsimd.tensor_tensor(
-                    out=product[:, lines].rearrange("p i j (gl c) -> p i (j gl) c", gl=2),
-                    in0=spread_rows[:, source_lines],
-                    in1=taps[:, dy, OWN_DX, lines].unsqueeze(3).to_broadcast([P, rows, 2 * SIDE, SHARE]),
-                    op=ALU.mult,
-                )
-                late.append((lines, product))
-                own = [dx for dx in range(TAPS) if dx != OWN_DX]
+                for dx, lag in lags.items():
+                    if dx not in gpsimd_columns(index, dy):
+                        continue
+                    j0, columns = inside(dx)
+                    product = products[dx][turn % len(products[dx])]
+                    s0 = 2 * (j0 + dx - REACH)
+                    nc.gpsimd.tensor_tensor(
+                        out=product[:, lines, j0 : j0 + columns].rearrange("p i j (gl c) -> p i (j gl) c", gl=2),
+                        in0=spread_rows[:, source_lines, s0 : s0 + 2 * columns],
+                        in1=taps[:, dy, dx, lines, 2 * j0 : 2 * (j0 + columns)]
+                        .unsqueeze(3)
+                        .to_broadcast([P, rows, 2 * columns, SHARE]),
+                        op=ALU.mult,
+                    )
+                    late.append((dy + lag, lines, product))
+                own = [dx for dx in range(TAPS) if dx not in gpsimd_columns(index, dy)]
                 for dx in own[::-1] if turn // SPARE % 2 else own:
                     j0, columns = inside(dx)
                     product = products[dx][turn % SPARE]
@@ -331,81 +363,88 @@ def tile_sam_pb_kernel(tc, logits, x, w3c, b3c, out):
                             op=ALU.mult,
                         )
                     add(lines, product)
-                if dy >= LAG:
-                    add(*late.pop(0))
+                for due, some, product in late:
+                    if due == dy:
+                        add(some, product)
                 between(dy)
-            for some in late:
-                add(*some)
+            for due, some, product in late:
+                if due >= TAPS:
+                    add(some, product)
             return sums
 
         chunks = [(hh, t) for hh in range(2) for t in range(2)]
-        totals, ready, quantised, waiting = {}, {}, {0: [], 1: []}, []
+        totals, ready, waiting = {}, {}, []
         shifts, done = {}, {}
 
         def begin(index):
             most = largest(logit_tiles[index])
             shift = loads.tile([P, 2, SPOTS], F32)
             nc.vector.tensor_scalar(out=shift[:], in0=most[:, :, 0], scalar1=-1.0, scalar2=None, op0=ALU.mult)
-            total = ends.tile([P, P], F32, bufs=3)
-            shifts[index], totals[index], done[index] = shift, total, 0
+            shifts[index], done[index] = shift, 0
 
         def advance(index, until):
-            some = range(done[index], until)
-            place_exponentials(logit_tiles[index], shifts[index], weights[index % 3], totals[index], some)
+            place_exponentials(logit_tiles[index], shifts[index], weights[index % 3], range(done[index], until))
             done[index] = until
 
-        for c in range(AHEAD, SHARE):
-            channels.append(load_channel(0, c))
-        quantised[0].extend(quantised_channel(grouped.pop(0)) for c in range(2))
-        for c in range(2, SHARE):
-            copy, tag = (nc.scalar.copy, "acc") if c % 2 else (nc.vector.tensor_copy, "x3")
-            quantised[0].append(quantised_channel(turned_channel(channels[c], copy, tag)))
-            if c == 3:
-                totals[0] = numerator_sums(weights[0])
-        begin(1)
+        def sum_up(index):
+            both = psum.tile([P, P], F32, tag="aux")
+            places = weights[index % 3][:].rearrange("p (s l) -> p s l", l=STRIDE)
+            add_numerators(both, lambda tap: places[:, :, tap], slice(0, TAPS * TAPS))
+            totals[index] = numerator_sums(both)
+
+        totals[0] = numerator_sums(both)
         fold_rows(nc.vector, by_tap(weights[0]), "dx s")
-        fold_columns(nc.vector, by_tap(weights[0]), slice(0, SIDE), "dy i gl")
+        quantised[0].append(quantised_channel(grouped.pop(0)))
+        fold_columns(nc.vector, by_tap(weights[0]), "dy i gl")
+        quantised[0].append(quantised_channel(grouped.pop(0)))
         nc.scalar.copy(out=bias[:], in_=bias_bf[:])
         ready[0] = project(0, quantised[0])
         channels = [load_channel(1, c) for c in range(AHEAD)]
+        grouped.append(turned_channel(channels[0], "aux"))
 
-        advance(1, 32)
 
         def prepare(index, dy):
-            if index + 1 < len(chunks) and dy < 4:
-                start = 32 if index == 0 else 56
-                advance(index + 1, start + (2 * SPOTS - start) * (dy + 1) // 4)
-            if index + 2 < len(chunks) and dy == 2:
-                logit_tiles[index + 2] = load_logits(*chunks[index + 2])
-            if index + 2 < len(chunks) and dy >= 4:
+            soon, later = index + 1, index + 2
+            if index == 0 and dy == 0:
+                begin(soon)
+                logit_tiles[2] = load_logits(*chunks[2])
+            if index == 0 and dy == 3:
+                logit_tiles[3] = load_logits(*chunks[3])
+            if soon < len(chunks):
+                places = (43, 86, 128) if index == 0 else (103, 128)
+                if dy < len(places):
+                    advance(soon, places[dy])
+                if dy == len(places):
+                    sum_up(soon)
+                turn = dy - len(places)
+                taps = by_place(weights[soon % 3])
+                if turn in (0, 1):
+                    fold_rows(nc.gpsimd, taps, "s dx", slice(6 * turn, 6 * turn + 6))
+                if turn in (2, 3):
+                    fold_columns(nc.gpsimd, taps, "i gl dy", slice(6 * turn - 12, 6 * turn - 6))
+            if later < len(chunks) and dy >= 4:
                 if dy == 4:
-                    begin(index + 2)
-                advance(index + 2, (19, 38, 56)[dy - 4])
-            if index + 1 < len(chunks):
-                taps = by_place(weights[(index + 1) % 3])
-                if dy == 4:
-                    fold_rows(nc.gpsimd, taps, "s dx")
-                if dy == 5:
-                    fold_columns(nc.gpsimd, taps, slice(0, SIDE), "i gl dy")
+                    begin(later)
+                advance(later, 26 * (dy - 3))
 
         for index, (hh, t) in enumerate(chunks):
 
             def between(dy):
-                if dy == 0 and waiting:
-                    finish(*waiting.pop())
+                if index > 0 and dy == 0:
+                    waiting.append(turn_back(waiting.pop()))
+                if index > 0 and dy == 1:
+                    finish(*chunks[index - 1], waiting.pop(), totals[index - 1])
                 if index + 1 < len(chunks):
                     if dy == (0 if index == 0 else 3):
                         ready[index + 1] = project(chunks[index + 1][1], quantised[chunks[index + 1][0]])
                 prepare(index, dy)
-                step = TAPS * index + dy - 1
-                if 1 <= step <= SHARE:
+                if grouped:
                     quantised[1].append(quantised_channel(grouped.pop(0)))
-                if 0 <= step < SHARE:
-                    if step + AHEAD < SHARE:
-                        channels.append(load_channel(1, step + AHEAD))
-                    grouped.append(turned_channel(channels[step], nc.scalar.copy, "aux"))
+                if index == 0:
+                    if len(channels) < SHARE:
+                        channels.append(load_channel(1, len(channels)))
+                    grouped.append(turned_channel(channels[dy + 1], "aux"))
 
             taps = by_place(weights[index % 3]) if index else by_tap(weights[0])
-            sums = window_sum(index, taps, *ready[index], between)
-            waiting.append((hh, t, sums, totals[index]))
-        finish(*waiting.pop())
+            waiting.append(window_sum(index, taps, *ready[index], between))
+        finish(*chunks[3], turn_back(waiting.pop()), totals[3])

@@ -42,7 +42,7 @@ def inside(d):
 
 
 def gpsimd_columns(index, dy):
-    helps = {0: (0, 1, 2), 3: range(TAPS)}.get(index, (0, 1, 6))
+    helps = {0: (0, 1, 2), 3: (0, 1, 2, 3, 4)}.get(index, ())
     return (HELP_DX, OWN_DX) if dy in helps else (OWN_DX,)
 
 
@@ -58,14 +58,11 @@ def tile_sam_pb_kernel(tc, logits, x, w3c, b3c, out):
         ident = keep.tile([P, P], F32)
         make_identity(nc, ident[:])
 
-        weights = [keep.tile([P, 2 * SPOTS * STRIDE], F32, name="weights%d" % r) for r in range(3)]
+        weights = [keep.tile([P, TAPS * TAPS * 2 * SPOTS], F32, name="weights%d" % r) for r in range(2)]
+        scratch = keep.tile([P, 2 * SPOTS, STRIDE], F32)
 
         def by_tap(e):
-            return e[:, 0 : TAPS * TAPS * 2 * SPOTS].rearrange("p (dy dx i s) -> p dy dx i s", dy=TAPS, dx=TAPS, i=SIDE)
-
-        def by_place(e):
-            places = e[:].rearrange("p (i s l) -> p i s l", i=SIDE, l=STRIDE)[:, :, :, 0 : TAPS * TAPS]
-            return places.rearrange("p i s (dy dx) -> p dy dx i s", dx=TAPS)
+            return e[:].rearrange("p (dy dx i s) -> p dy dx i s", dy=TAPS, dx=TAPS, i=SIDE)
 
         def load_logits(hh, t):
             lt = loads.tile([P, 2, TAPS * TAPS, SPOTS], BF16)
@@ -103,15 +100,22 @@ def tile_sam_pb_kernel(tc, logits, x, w3c, b3c, out):
             )
             nc.scalar.activation(out=some, in_=some, func=ACT.Exp)
 
-        def place_exponentials(lt, shift, e, places):
+        def place_exponentials(lt, shift, total, places):
             for place in places:
                 n, gl = divmod(place, 2)
                 nc.scalar.activation(
-                    out=e[:, place * STRIDE : place * STRIDE + TAPS * TAPS],
+                    out=scratch[:, place, 0 : TAPS * TAPS],
                     in_=lt[:, gl, :, n],
                     func=ACT.Exp,
                     bias=shift[:, gl, n : n + 1],
+                    accum_out=total[:, place : place + 1],
                 )
+
+        def lay_by_tap(e, part):
+            nc.scalar.copy(
+                out=e[:, part.start * 2 * SPOTS : part.stop * 2 * SPOTS].rearrange("p (l s) -> p l s", s=2 * SPOTS),
+                in_=scratch[:, :, part].rearrange("p s l -> p l s"),
+            )
 
         folds = []
         for s in range(SIDE):
@@ -120,16 +124,14 @@ def tile_sam_pb_kernel(tc, logits, x, w3c, b3c, out):
                 if mirrored(u) != u:
                     folds.append((s, d, mirrored(u) - s + REACH))
 
-        def fold_rows(engine, taps, order, some=slice(0, 12)):
-            for i, dy, twin_dy in folds[some]:
-                twin, own = [taps[:, d, :, i].rearrange("p dx s -> p " + order) for d in (twin_dy, dy)]
+        def fold_rows(engine, taps):
+            for i, dy, twin_dy in folds:
+                twin, own = [taps[:, d, :, i] for d in (twin_dy, dy)]
                 engine.tensor_tensor(out=twin, in0=twin, in1=own, op=ALU.add)
 
-        def fold_columns(engine, taps, order, some=slice(0, 12)):
+        def fold_columns(engine, taps, some=slice(0, 12)):
             for j, dx, twin_dx in folds[some]:
-                twin, own = [
-                    taps[:, :, d, :, 2 * j : 2 * j + 2].rearrange("p dy i gl -> p " + order) for d in (twin_dx, dx)
-                ]
+                twin, own = [taps[:, :, d, :, 2 * j : 2 * j + 2] for d in (twin_dx, dx)]
                 engine.tensor_tensor(out=twin, in0=twin, in1=own, op=ALU.add)
 
         w_view = w3c.rearrange("(hh k c) q -> hh k c q", hh=2, k=P, c=SHARE)
@@ -162,11 +164,11 @@ def tile_sam_pb_kernel(tc, logits, x, w3c, b3c, out):
             )
             return codes_w, scales_w
 
-        def add_numerators(both, taps_of, part):
+        def add_numerators(both, e, part):
             for tap in range(part.start, part.stop):
                 nc.tensor.matmul(
                     out=both[:],
-                    lhsT=taps_of(tap),
+                    lhsT=e[:, tap * 2 * SPOTS : (tap + 1) * 2 * SPOTS],
                     rhs=ident[:],
                     is_transpose=True,
                     start=(tap == 0),
@@ -199,7 +201,7 @@ def tile_sam_pb_kernel(tc, logits, x, w3c, b3c, out):
                 if step == 3:
                     channels.append(load_channel(0, 3))
                 grouped.append(turned_channel(channels[step], "acc" if step == 2 else "x3"))
-                add_numerators(both, lambda tap: weights[0][:, tap * 2 * SPOTS : (tap + 1) * 2 * SPOTS], part)
+                add_numerators(both, weights[0], part)
             grouped_x = once.tile([P, 4, 2, SPOTS, 2, 4], BF16, align_bytes=64)
             raw_view = raw_x[:].rearrange("p (t gl g u) (e n) -> p g t n gl (u e)", t=2, gl=2, g=4, u=2, e=2)
             for g in range(4):
@@ -380,52 +382,54 @@ def tile_sam_pb_kernel(tc, logits, x, w3c, b3c, out):
             most = largest(logit_tiles[index])
             shift = loads.tile([P, 2, SPOTS], F32)
             nc.vector.tensor_scalar(out=shift[:], in0=most[:, :, 0], scalar1=-1.0, scalar2=None, op0=ALU.mult)
-            shifts[index], done[index] = shift, 0
+            total = ends.tile([P, P], F32, bufs=3)
+            shifts[index], totals[index], done[index] = shift, total, 0
 
         def advance(index, until):
-            place_exponentials(logit_tiles[index], shifts[index], weights[index % 3], range(done[index], until))
+            place_exponentials(logit_tiles[index], shifts[index], totals[index], range(done[index], until))
             done[index] = until
 
         def sum_up(index):
             both = psum.tile([P, P], F32, tag="aux")
-            places = weights[index % 3][:].rearrange("p (s l) -> p s l", l=STRIDE)
-            add_numerators(both, lambda tap: places[:, :, tap], slice(0, TAPS * TAPS))
+            add_numerators(both, weights[index % 2], slice(0, TAPS * TAPS))
             totals[index] = numerator_sums(both)
 
         totals[0] = numerator_sums(both)
-        fold_rows(nc.vector, by_tap(weights[0]), "dx s")
+        fold_rows(nc.vector, by_tap(weights[0]))
         quantised[0].append(quantised_channel(grouped.pop(0)))
-        fold_columns(nc.vector, by_tap(weights[0]), "dy i gl")
+        fold_columns(nc.vector, by_tap(weights[0]))
         quantised[0].append(quantised_channel(grouped.pop(0)))
         nc.scalar.copy(out=bias[:], in_=bias_bf[:])
         ready[0] = project(0, quantised[0])
         channels = [load_channel(1, c) for c in range(AHEAD)]
         grouped.append(turned_channel(channels[0], "aux"))
 
+        parts = [slice(TAPS * dy, TAPS * dy + TAPS) for dy in range(TAPS)]
 
         def prepare(index, dy):
             soon, later = index + 1, index + 2
             if index == 0 and dy == 0:
-                begin(soon)
+                tops[1] = largest(logit_tiles[1])
                 logit_tiles[2] = load_logits(*chunks[2])
+            if index == 0 and dy < 2:
+                for part in (slice(0, 24), slice(24, 49))[dy : dy + 1]:
+                    shifted_exponentials(logit_tiles[1], tops[1], weights[1], part)
             if index == 0 and dy == 3:
                 logit_tiles[3] = load_logits(*chunks[3])
+            if index in (1, 2) and dy < 2:
+                for part in (parts[0:4], parts[4:7])[dy]:
+                    lay_by_tap(weights[soon % 2], part)
             if soon < len(chunks):
-                places = (43, 86, 128) if index == 0 else (103, 128)
-                if dy < len(places):
-                    advance(soon, places[dy])
-                if dy == len(places):
-                    sum_up(soon)
-                turn = dy - len(places)
-                taps = by_place(weights[soon % 3])
-                if turn in (0, 1):
-                    fold_rows(nc.gpsimd, taps, "s dx", slice(6 * turn, 6 * turn + 6))
-                if turn in (2, 3):
-                    fold_columns(nc.gpsimd, taps, "i gl dy", slice(6 * turn - 12, 6 * turn - 6))
-            if later < len(chunks) and dy >= 4:
-                if dy == 4:
+                if dy == 2:
+                    if soon == 1:
+                        sum_up(soon)
+                    fold_rows(nc.gpsimd, by_tap(weights[soon % 2]))
+                if dy in (3, 4):
+                    fold_columns(nc.gpsimd, by_tap(weights[soon % 2]), slice(6 * dy - 18, 6 * dy - 12))
+            if later < len(chunks) and dy >= 2:
+                if dy == 2:
                     begin(later)
-                advance(later, 26 * (dy - 3))
+                advance(later, 2 * SPOTS * (dy - 1) // 5)
 
         for index, (hh, t) in enumerate(chunks):
 
@@ -445,6 +449,5 @@ def tile_sam_pb_kernel(tc, logits, x, w3c, b3c, out):
                         channels.append(load_channel(1, len(channels)))
                     grouped.append(turned_channel(channels[dy + 1], "aux"))
 
-            taps = by_place(weights[index % 3]) if index else by_tap(weights[0])
-            waiting.append(window_sum(index, taps, *ready[index], between))
+            waiting.append(window_sum(index, by_tap(weights[index % 2]), *ready[index], between))
         finish(*chunks[3], turn_back(waiting.pop()), totals[3])

from contextlib import ExitStack

import concourse.mybir as mybir
from concourse.masks import make_identity

F32 = mybir.dt.float32
BF16 = mybir.dt.bfloat16
U32 = mybir.dt.uint32
U8 = mybir.dt.uint8
FP8X4 = mybir.dt.float8_e4m3fn_x4
ALU = mybir.AluOpType
ACT = mybir.ActivationFunctionType

P = 128
SIDE = 8
SPOTS = SIDE * SIDE
TAPS = 7
REACH = TAPS // 2
SHARE = 8
HALF = SHARE // 2
SPARE = 2
OWN_DX = REACH
AHEAD = 3
HELP_DX = 2
LAG = 2
STRIDE = 52
BANKS = {"x3": 4, "acc": 2, "aux": 2}
FLOPS = 2 * 2048 * 2048 * 256 + 2 * 4 * 2048 * 64 * 49


def mirrored(u):
    if u < 0:
        return -u
    if u > SIDE - 1:
        return 2 * (SIDE - 1) - u
    return u


def inside(d):
    first = max(0, REACH - d)
    return first, min(SIDE, SIDE + REACH - d) - first


def gpsimd_columns(index, dy):
    helps = {0: (0, 1, 2), 3: (0, 1, 2, 3, 4)}.get(index, ())
    return (HELP_DX, OWN_DX) if dy in helps else (OWN_DX,)


def tile_sam_pb_kernel(tc, logits, x, w3c, b3c, out):
    nc = tc.nc
    with ExitStack() as stack:
        stack.enter_context(tc.manual_schedule())
        keep = stack.enter_context(tc.tile_pool(name="keep", bufs=1))
        loads = stack.enter_context(tc.tile_pool(name="loads", bufs=2))
        stream = stack.enter_context(tc.tile_pool(name="stream", bufs=2))
        psum = stack.enter_context(tc.psum_pool(name="psum", bufs=2))

        ident = keep.tile([P, P], F32)
        make_identity(nc, ident[:])

        weights = [keep.tile([P, TAPS * TAPS * 2 * SPOTS], F32, name="weights%d" % r) for r in range(2)]
        scratch = keep.tile([P, 2 * SPOTS, STRIDE], F32)

        def by_tap(e):
            return e[:].rearrange("p (dy dx i s) -> p dy dx i s", dy=TAPS, dx=TAPS, i=SIDE)

        def load_logits(hh, t):
            lt = loads.tile([P, 2, TAPS * TAPS, SPOTS], BF16)
            for gl in range(2):
                nc.sync.dma_start(out=lt[:, gl], in_=logits[2 * t + gl, hh * P : (hh + 1) * P])
            return lt

        def largest(lt):
            top = keep.tile([P, 2, 24, SPOTS], BF16)
            most = loads.tile([P, 2, 1, SPOTS], BF16)
            nc.vector.tensor_tensor(out=top[:], in0=lt[:, :, 0:24, :], in1=lt[:, :, 24:48, :], op=ALU.max)
            width = 24
            while width > 1:
                half = width // 2
                nc.vector.tensor_tensor(
                    out=top[:, :, 0:half, :],
                    in0=top[:, :, 0:half, :],
                    in1=top[:, :, width - half : width, :],
                    op=ALU.max,
                )
                width -= half
            nc.vector.tensor_tensor(
                out=most[:], in0=top[:, :, 0:1, :], in1=lt[:, :, 48:49, :], op=ALU.max
            )
            return most

        def shifted_exponentials(lt, most, e, part):
            count = part.stop - part.start
            some = e[:, part.start * 2 * SPOTS : part.stop * 2 * SPOTS]
            nc.vector.tensor_tensor(
                out=some.rearrange("p (l n gl) -> p l n gl", l=count, gl=2),
                in0=lt[:, :, part].rearrange("p gl l n -> p l n gl"),
                in1=most[:, :, 0].rearrange("p gl n -> p n gl").unsqueeze(1).to_broadcast([P, count, SPOTS, 2]),
                op=ALU.subtract,
            )
            nc.scalar.activation(out=some, in_=some, func=ACT.Exp)

        def place_exponentials(lt, shift, total, places):
            for place in places:
                n, gl = divmod(place, 2)
                nc.scalar.activation(
                    out=scratch[:, place, 0 : TAPS * TAPS],
                    in_=lt[:, gl, :, n],
                    func=ACT.Exp,
                    bias=shift[:, gl, n : n + 1],
                    accum_out=total[:, place : place + 1],
                )

        def lay_by_tap(e, part):
            nc.scalar.copy(
                out=e[:, part.start * 2 * SPOTS : part.stop * 2 * SPOTS].rearrange("p (l s) -> p l s", s=2 * SPOTS),
                in_=scratch[:, :, part].rearrange("p s l -> p l s"),
            )

        folds = []
        for s in range(SIDE):
            for d in range(TAPS):
                u = s + d - REACH
                if mirrored(u) != u:
                    folds.append((s, d, mirrored(u) - s + REACH))

        def fold_rows(engine, taps):
            for i, dy, twin_dy in folds:
                twin, own = [taps[:, d, :, i] for d in (twin_dy, dy)]
                engine.tensor_tensor(out=twin, in0=twin, in1=own, op=ALU.add)

        def fold_columns(engine, taps, some=slice(0, 12)):
            for j, dx, twin_dx in folds[some]:
                twin, own = [taps[:, :, d, :, 2 * j : 2 * j + 2] for d in (twin_dx, dx)]
                engine.tensor_tensor(out=twin, in0=twin, in1=own, op=ALU.add)

        w_view = w3c.rearrange("(hh k c) q -> hh k c q", hh=2, k=P, c=SHARE)

        def load_channel(hh, c):
            w_sb = stream.tile([P, 2048], BF16, bufs=AHEAD)
            nc.sync.dma_start(out=w_sb[:], in_=w_view[hh][:, c, :])
            return w_sb

        def turned_channel(w_sb, tag):
            words = w_sb[:].bitcast(F32)
            grouped_w = stream.tile([P, 4, P, 4], BF16, align_bytes=64)
            for pair in range(2):
                wt = psum.tile([P, 2, 2, P], F32, tag=tag, bufs=BANKS[tag])
                for gl in range(2):
                    for u in range(2):
                        q = 2 * (2 * pair + gl) + u
                        nc.tensor.transpose(wt[:, gl, u, :], words[:, q * P : (q + 1) * P], ident[:])
                some = grouped_w[:, 2 * pair : 2 * pair + 2].rearrange("p g o f -> p g (o f)").bitcast(F32)
                nc.scalar.copy(out=some.rearrange("p g (o u) -> p g o u", u=2), in_=wt[:].rearrange("p g u o -> p g o u"))
            return grouped_w

        def quantised_channel(grouped_w):
            codes_w = stream.tile([P, 4, P], U32, align_bytes=64, bufs=SHARE)
            scales_w = stream.tile([P, 4, P], U8, align_bytes=64, bufs=SHARE)
            nc.vector.quantize_mx(
                out=codes_w[:].rearrange("p g o -> p (g o)").bitcast(FP8X4),
                scales=scales_w[:].rearrange("p g o -> p (g o)"),
                in_=grouped_w[:].rearrange("p g o f -> p (g o f)"),
            )
            return codes_w, scales_w

        def add_numerators(both, e, part):
            for tap in range(part.start, part.stop):
                nc.tensor.matmul(
                    out=both[:],
                    lhsT=e[:, tap * 2 * SPOTS : (tap + 1) * 2 * SPOTS],
                    rhs=ident[:],
                    is_transpose=True,
                    start=(tap == 0),
                    stop=(tap == TAPS * TAPS - 1),
                )

        logit_tiles = {0: load_logits(0, 0)}
        tops = {0: largest(logit_tiles[0])}
        bias_bf = keep.tile([P, 2, SHARE], BF16)
        bias = keep.tile([P, 2, SHARE], F32)

        codes_x = keep.tile([P, 4, 256], U32, align_bytes=64)
        scales_x = keep.tile([P, 4, 256], U8, align_bytes=64)
        with tc.tile_pool(name="once", bufs=1) as once:
            raw_x = once.tile([P, 32, 128], BF16)
            nc.sync.dma_start(
                out=raw_x[:],
                in_=x.rearrange("b (g u p e) i j -> p (b g u) (e i j)", g=4, u=2, p=P, e=2),
            )
            channels = [load_channel(0, c) for c in range(AHEAD)]
            logit_tiles[1] = load_logits(0, 1)
            nc.sync.dma_start(out=bias_bf[:], in_=b3c.rearrange("(hh k c) -> k hh c", hh=2, k=P, c=SHARE))
            both = psum.tile([P, P], F32, tag="aux")
            grouped = []
            quantised = {0: [], 1: []}
            for step, part in enumerate((slice(0, 12), slice(12, 24), slice(24, 36), slice(36, 49))):
                shifted_exponentials(logit_tiles[0], tops[0], weights[0], part)
                if step >= 2:
                    quantised[0].append(quantised_channel(grouped.pop(0)))
                if step == 3:
                    channels.append(load_channel(0, 3))
                grouped.append(turned_channel(channels[step], "acc" if step == 2 else "x3"))
                add_numerators(both, weights[0], part)
            grouped_x = once.tile([P, 4, 2, SPOTS, 2, 4], BF16, align_bytes=64)
            raw_view = raw_x[:].rearrange("p (t gl g u) (e n) -> p g t n gl (u e)", t=2, gl=2, g=4, u=2, e=2)
            for g in range(4):
                for t in range(2):
                    nc.vector.tensor_copy(out=grouped_x[:, g, t], in_=raw_view[:, g, t])
                if g % 2 == 1:
                    for c in range(2):
                        quantised[0].append(quantised_channel(grouped.pop(0)))
                        channels.append(load_channel(0, len(channels)))
                        grouped.append(turned_channel(channels[-1], "acc" if c else "x3"))
            nc.vector.quantize_mx(
                out=codes_x[:].rearrange("p g n -> p (g n)").bitcast(FP8X4),
                scales=scales_x[:].rearrange("p g n -> p (g n)"),
                in_=grouped_x[:].rearrange("p g t n gl f -> p (g t n gl f)"),
            )
        flow = stack.enter_context(tc.tile_pool(name="flow", bufs=1))
        ends = stack.enter_context(tc.tile_pool(name="ends", bufs=2))

        products = {}
        for dx in range(TAPS):
            first, count = inside(dx)
            products[dx] = [
                flow.tile([P, SIDE, SIDE, 2 * SHARE], F32, name="product%d_%d" % (dx, s))
                for s in range(LAG + 1 if dx == OWN_DX else SPARE)
            ]
            for spare in products[dx]:
                if first > 0:
                    nc.gpsimd.memset(spare[:, :, 0:first, :], 0.0)
                if first + count < SIDE:
                    nc.gpsimd.memset(spare[:, :, first + count : SIDE, :], 0.0)

        def project(t, quantised):
            spread = ends.tile([P, SPOTS * 2, SHARE], F32)
            banks = []
            columns = slice(t * P, (t + 1) * P)
            for half in range(2):
                bank = psum.tile([P, HALF, P], F32, tag="x3", bufs=BANKS["x3"])
                for r in range(HALF):
                    c = half * HALF + r
                    codes_w, scales_w = quantised[c]
                    for g in range(4):
                        nc.tensor.matmul_mx(
                            out=bank[:, r, :],
                            lhsT=codes_w[:, g, :].bitcast(FP8X4),
                            lhsT_scale=scales_w[:, g, :],
                            rhs=codes_x[:, g, columns].bitcast(FP8X4),
                            rhs_scale=scales_x[:, g, columns],
                            start=(g == 0),
                            stop=(g == 3),
                        )
                nc.scalar.copy(
                    out=spread[:, :, half * HALF : (half + 1) * HALF], in_=bank[:].rearrange("p c s -> p s c")
                )
                banks.append(bank)
            return banks, spread

        out_view = out.rearrange("b (hh k c) i j -> hh k b c (i j)", hh=2, k=P, c=SHARE)

        def numerator_sums(both):
            turned_sum = ends.tile([P, P], F32)
            nc.scalar.copy(out=turned_sum[:], in_=both[:])
            again = psum.tile([P, P], F32, tag="aux")
            nc.tensor.transpose(again[:], turned_sum[:], ident[:])
            total = ends.tile([P, P], F32, bufs=3)
            nc.scalar.copy(out=total[:], in_=again[:])
            return total

        def turn_back(sums):
            turned = ends.tile([P, SIDE, P], F32, bufs=1)
            for bank in range(2):
                nc.scalar.copy(
                    out=turned[:].rearrange("p (h bank) k -> p bank h k", bank=2)[:, bank], in_=sums[bank][:]
                )
            backs = []
            for half in range(2):
                back = psum.tile([P, 4, SIDE, 2, SHARE], F32, tag="aux")
                for r in range(4):
                    nc.tensor.transpose(
                        back[:, r].rearrange("p j gl c -> p (j gl c)"), turned[:, 4 * half + r, :], ident[:]
                    )
                backs.append(back)
            return backs

        def finish(hh, t, backs, total):
            rec = ends.tile([P, SIDE, SIDE, 2], F32)
            nc.vector.reciprocal(out=rec[:].rearrange("p i j gl -> p (i j gl)"), in_=total[:])
            result = ends.tile([P, 2, SHARE, SIDE, SIDE], F32, bufs=1)
            for gl in range(2):
                for half in range(2):
                    some = slice(4 * half, 4 * half + 4)
                    nc.vector.tensor_tensor(
                        out=result[:, gl, :, some, :],
                        in0=backs[half][:, :, :, gl].rearrange("p i j c -> p c i j"),
                        in1=rec[:, some, :, gl].unsqueeze(1).to_broadcast([P, SHARE, 4, SIDE]),
                        op=ALU.mult,
                    )
                for c in range(SHARE):
                    lane = result[:, gl, c].rearrange("p i j -> p (i j)")
                    nc.scalar.activation(out=lane, in_=lane, func=ACT.Identity, bias=bias[:, hh, c : c + 1])
                nc.sync.dma_start(
                    out=out_view[hh, :, 2 * t + gl], in_=result[:, gl].rearrange("p c i j -> p c (i j)")
                )

        def window_sum(index, taps, banks, spread, between):
            sources = [bank[:].rearrange("p c (i s) -> p i s c", i=SIDE) for bank in banks]
            spread_rows = spread[:].rearrange("p (i s) c -> p i s c", i=SIDE)
            sums = [psum.tile([P, SIDE // 2, P], F32, tag="acc", name="sums%d" % bank) for bank in range(2)]
            opened = set()
            left = [TAPS * sum(inside(dy)[1] for dy in range(TAPS)) // 2] * 2

            def add(lines, product):
                for i in range(lines.start, lines.stop):
                    bank = i % 2
                    left[bank] -= 1
                    nc.tensor.matmul(
                        out=sums[bank][:, i // 2, :],
                        lhsT=product[:, i].rearrange("p j s -> p (j s)"),
                        rhs=ident[:],
                        is_transpose=True,
                        start=(bank not in opened),
                        stop=(left[bank] == 0),
                    )
                    opened.add(bank)

            late = []
            lags = {OWN_DX: LAG, HELP_DX: 1}
            for dy in range(TAPS):
                i0, rows = inside(dy)
                lines = slice(i0, i0 + rows)
                source_lines = slice(i0 + dy - REACH, i0 + dy - REACH + rows)
                turn = TAPS * index + dy
                for dx, lag in lags.items():
                    if dx not in gpsimd_columns(index, dy):
                        continue
                    j0, columns = inside(dx)
                    product = products[dx][turn % len(products[dx])]
                    s0 = 2 * (j0 + dx - REACH)
                    nc.gpsimd.tensor_tensor(
                        out=product[:, lines, j0 : j0 + columns].rearrange("p i j (gl c) -> p i (j gl) c", gl=2),
                        in0=spread_rows[:, source_lines, s0 : s0 + 2 * columns],
                        in1=taps[:, dy, dx, lines, 2 * j0 : 2 * (j0 + columns)]
                        .unsqueeze(3)
                        .to_broadcast([P, rows, 2 * columns, SHARE]),
                        op=ALU.mult,
                    )
                    late.append((dy + lag, lines, product))
                own = [dx for dx in range(TAPS) if dx not in gpsimd_columns(index, dy)]
                for dx in own[::-1] if turn // SPARE % 2 else own:
                    j0, columns = inside(dx)
                    product = products[dx][turn % SPARE]
                    s0, s1 = 2 * (j0 + dx - REACH), 2 * (j0 + dx - REACH + columns)
                    for half in range(2):
                        nc.vector.tensor_tensor(
                            out=product[:, lines, j0 : j0 + columns].rearrange("p i j (gl c) -> p i (j gl) c", gl=2)[
                                :, :, :, half * HALF : (half + 1) * HALF
                            ],
                            in0=sources[half][:, source_lines, s0:s1],
                            in1=taps[:, dy, dx, lines, 2 * j0 : 2 * (j0 + columns)]
                            .unsqueeze(3)
                            .to_broadcast([P, rows, 2 * columns, HALF]),
                            op=ALU.mult,
                        )
                    add(lines, product)
                for due, some, product in late:
                    if due == dy:
                        add(some, product)
                between(dy)
            for due, some, product in late:
                if due >= TAPS:
                    add(some, product)
            return sums

        chunks = [(hh, t) for hh in range(2) for t in range(2)]
        totals, ready, waiting = {}, {}, []
        shifts, done = {}, {}

        def begin(index):
            most = largest(logit_tiles[index])
            shift = loads.tile([P, 2, SPOTS], F32)
            nc.vector.tensor_scalar(out=shift[:], in0=most[:, :, 0], scalar1=-1.0, scalar2=None, op0=ALU.mult)
            total = ends.tile([P, P], F32, bufs=3)
            shifts[index], totals[index], done[index] = shift, total, 0

        def advance(index, until):
            place_exponentials(logit_tiles[index], shifts[index], totals[index], range(done[index], until))
            done[index] = until

        def sum_up(index):
            both = psum.tile([P, P], F32, tag="aux")
            add_numerators(both, weights[index % 2], slice(0, TAPS * TAPS))
            totals[index] = numerator_sums(both)

        totals[0] = numerator_sums(both)
        fold_rows(nc.vector, by_tap(weights[0]))
        quantised[0].append(quantised_channel(grouped.pop(0)))
        fold_columns(nc.vector, by_tap(weights[0]))
        quantised[0].append(quantised_channel(grouped.pop(0)))
        nc.scalar.copy(out=bias[:], in_=bias_bf[:])
        ready[0] = project(0, quantised[0])
        channels = [load_channel(1, c) for c in range(AHEAD)]
        grouped.append(turned_channel(channels[0], "aux"))

        parts = [slice(TAPS * dy, TAPS * dy + TAPS) for dy in range(TAPS)]

        def prepare(index, dy):
            soon, later = index + 1, index + 2
            if index == 0 and dy == 0:
                tops[1] = largest(logit_tiles[1])
                logit_tiles[2] = load_logits(*chunks[2])
            if index == 0 and dy < 2:
                for part in (slice(0, 24), slice(24, 49))[dy : dy + 1]:
                    shifted_exponentials(logit_tiles[1], tops[1], weights[1], part)
            if index == 0 and dy == 3:
                logit_tiles[3] = load_logits(*chunks[3])
            if index in (1, 2) and dy < 2:
                for part in (parts[0:4], parts[4:7])[dy]:
                    lay_by_tap(weights[soon % 2], part)
            if soon < len(chunks):
                if dy == 2:
                    if soon == 1:
                        sum_up(soon)
                    fold_rows(nc.gpsimd, by_tap(weights[soon % 2]))
                if dy in (3, 4):
                    fold_columns(nc.gpsimd, by_tap(weights[soon % 2]), slice(6 * dy - 18, 6 * dy - 12))
            if later < len(chunks) and dy >= 2:
                if dy == 2:
                    begin(later)
                advance(later, 2 * SPOTS * (dy - 1) // 5)

        for index, (hh, t) in enumerate(chunks):

            def between(dy):
                if index > 0 and dy == 0:
                    waiting.append(turn_back(waiting.pop()))
                if index > 0 and dy == 1:
                    finish(*chunks[index - 1], waiting.pop(), totals[index - 1])
                if index + 1 < len(chunks):
                    if dy == (0 if index == 0 else 3):
                        ready[index + 1] = project(chunks[index + 1][1], quantised[chunks[index + 1][0]])
                prepare(index, dy)
                if grouped:
                    quantised[1].append(quantised_channel(grouped.pop(0)))
                if index == 0:
                    if len(channels) < SHARE:
                        channels.append(load_channel(1, len(channels)))
                    grouped.append(turned_channel(channels[dy + 1], "aux"))

            waiting.append(window_sum(index, by_tap(weights[index % 2]), *ready[index], between))
        finish(*chunks[3], turn_back(waiting.pop()), totals[3])
